import numpy as np
import ml_dtypes


def mxq(x, axis, fmt="e4m3"):
    dtype, down = {"e4m3": (ml_dtypes.float8_e4m3fn, 7), "e5m2": (ml_dtypes.float8_e5m2, 14)}[fmt]
    v = np.moveaxis(np.asarray(x, np.float32).astype(ml_dtypes.bfloat16).astype(np.float64), axis, -1)
    blocks = v.reshape(v.shape[:-1] + (-1, 32))
    amax = np.abs(blocks).max(-1, keepdims=True)
    byte = np.maximum(np.where(amax > 0, np.frexp(amax)[1] - 1 + 127, 0) - down, 1)
    scale = np.exp2(byte - 127.0)
    codes = (blocks / scale).astype(np.float32).astype(dtype).astype(np.float64)
    return np.moveaxis((codes * scale).reshape(v.shape), -1, axis)


WIDE = False


def mx_kscale(k):
    if not WIDE:
        return np.ones(k)
    levels = np.array([10, -10, 5, -5, 0])
    if k % 512:
        return np.exp2(np.random.permutation(np.resize(levels, k // 32))).repeat(32)
    a = np.empty((k // 512, 16))
    for p in range(k // 512):
        a[p, :8] = np.random.permutation(np.resize(levels, 8))
        for g in range(8):
            far = levels[np.abs(levels - a[p, g]) >= 10]
            a[p, g + 8] = far[np.random.randint(len(far))]
    return np.exp2(a.ravel()).repeat(32)


BF16 = ml_dtypes.bfloat16


def bf(x):
    return np.asarray(x, np.float32).astype(BF16)


def f64(x):
    return np.asarray(x).astype(np.float64)


B, Nb1, Nw1, Nb2x, Nb2y, Nw2x, Nw2y, R, C = 128, 4, 16, 4, 2, 16, 16, 128, 2
J1 = Nb1 * Nb1
K1 = C * Nw1 * Nw1
J3 = Nb2x * Nb2y
L1 = J3 * R
J2 = J3 * J1


def draw0():
    s = mx_kscale(K1)
    sx = s.reshape(Nw1, Nw1, C)[:, None, :, :]
    x = np.random.standard_normal((B, Nb1, Nw1, Nb1, Nw1, C)) * sx
    return {"x": bf(x.reshape(B, Nb1 * Nw1 * Nb1 * Nw1, C)),
            "k1": bf(np.random.standard_normal((J1, K1, L1)) / np.sqrt(K1) / s[None, :, None]),
            "b1": bf(np.random.standard_normal((1, J1, L1)) * 0.3)}


def core(x, k1, b1):
    h = f64(x).reshape(B, Nb1, Nw1, Nb1, Nw1, C).transpose(0, 1, 3, 2, 4, 5).reshape(B, J1, K1)
    hq = mxq(h, 2, "e4m3").transpose(1, 0, 2)
    y = (hq @ mxq(f64(k1), 1, "e4m3")).transpose(1, 0, 2) + f64(b1)
    y = y.reshape(B, J1, J3, R).transpose(0, 3, 1, 2)
    return y.reshape(B, J2, R)


def e4m3fn_bytes(y):
    return np.clip(np.asarray(y, np.float64), -448.0, 448.0).astype(np.float32).astype(ml_dtypes.float8_e4m3fn).view(np.uint8)


def e4m3fn_values(b):
    return np.asarray(b, np.uint8).view(ml_dtypes.float8_e4m3fn).astype(np.float64)


def setup_inputs():
    d = draw0()
    x0 = np.asarray(d['k1']).astype(np.float64)
    s = (np.max(np.abs(x0), axis=(0, 2), keepdims=True) / 448.0).astype(np.float32)
    out = {}
    for k, v in d.items():
        if k == 'k1':
            out['k1_bytes'] = e4m3fn_bytes(x0 / s.astype(np.float64))
            out['k1_scale'] = s
        else:
            out[k] = v
    return out


def reference(x, k1_bytes, k1_scale, b1):
    return core(x, e4m3fn_values(k1_bytes) * k1_scale.astype(np.float64), b1)

@@ -1,0 +1,259 @@
+from contextlib import ExitStack
+
+import concourse.masks as masks
+import concourse.mybir as mybir
+
+FLOPS = 2 * 128 * 16 * 512 * 1024
+
+F32 = mybir.dt.float32
+BF16 = mybir.dt.bfloat16
+U32 = mybir.dt.uint32
+U8 = mybir.dt.uint8
+FP8 = mybir.dt.float8_e4m3fn
+FP8X4 = mybir.dt.float8_e4m3fn_x4
+ACT = mybir.ActivationFunctionType
+ALU = mybir.AluOpType
+
+P = 128
+NJ = 16
+RC = 16
+NCHUNK = 128 // RC
+NUNIT = 2 * NCHUNK
+STAGE_BUFS = 4
+SIDE_BUFS = 4
+VJ = [4, 4, 3, 3, 2, 2, 2, 2, 2, 2, 2, 2, 2, 2, 1, 1]
+GJ = [0, 0, 0, 0, 1, 1, 1, 1, 1, 1, 1, 1, 1, 1, 1, 1]
+
+
+def tile_switchnet_fstar_pa_kernel(tc, x, k1_bytes, k1_scale, b1, out):
+    nc = tc.nc
+    with ExitStack() as ctx:
+        keep = ctx.enter_context(tc.tile_pool(name="keep", bufs=1))
+        work = ctx.enter_context(tc.tile_pool(name="work", bufs=2))
+        psum = ctx.enter_context(tc.psum_pool(name="psum", bufs=8))
+        ctx.enter_context(tc.manual_schedule())
+
+        planes_a = keep.tile([P, 4, 8192], BF16, name="planes_a")
+        planes_b = keep.tile([P, 4, 8192], BF16, name="planes_b")
+        planes = [planes_a, planes_b]
+        b_nat = keep.tile([P, P], BF16, name="b_nat")
+        b_f32 = keep.tile([P, P], F32, name="b_f32")
+        b_t = keep.tile([P, P], BF16, name="b_t")
+        hcodes = keep.tile([P, 2048], U32, name="hcodes", align_bytes=64)
+        hscl = keep.tile([P, 2048], U8, name="hscl", align_bytes=64)
+        ident = keep.tile([P, P], F32, name="ident")
+        sc = keep.tile([P, 4], F32, name="sc")
+        warm = keep.tile([P, 2], F32, name="warm")
+
+        nc.scalar.dma_start(out=sc[:], in_=k1_scale.rearrange("o (p t) x -> p (o t x)", t=4))
+        nc.scalar.dma_start(out=b_nat[:], in_=b1.rearrange("o j (m r) -> (o j m) r", r=128))
+        nc.vector.memset(warm[:], 0.0)
+        nc.scalar.activation(out=warm[:, 1:2], in_=warm[:, 0:1], func=ACT.Copy)
+        masks.make_identity(nc, ident[:])
+
+        scratch = out[127].rearrange("r q -> (r q)").bitcast(BF16)[0:16384]
+
+        def permute_bias():
+            for h in range(2):
+                cols = slice(h * 64, (h + 1) * 64)
+                nc.vector.tensor_copy(
+                    out=b_f32[:, cols].rearrange("q (c e i) -> q c e i", c=8, e=2, i=4),
+                    in_=b_nat[:, cols].rearrange("q (e c i) -> q c e i", e=2, c=8, i=4),
+                )
+            pb = psum.tile([P, 4, 128], F32, name="pb", tag="bank")
+            nc.tensor.transpose(out=pb[:, 0, :], in_=b_f32[:], identity=ident[:])
+            nc.scalar.copy(out=b_t[:], in_=pb[:, 0, :])
+            nc.scalar.dma_start(out=scratch.rearrange("(w q) -> w q", q=128), in_=b_t[:])
+
+        bias_c = {}
+
+        def load_bias(c):
+            bt = work.tile([P, 2048], BF16, name="bias_c", tag="bias_c", bufs=3, align_bytes=64)
+            nc.sync.dma_start(
+                out=bt[:].rearrange("b (h x) -> b h x", h=2),
+                in_=scratch.rearrange("(h c x) -> c h x", h=2, c=NCHUNK)[c].partition_broadcast(P),
+            )
+            bias_c[c] = bt
+
+        def stage_tile(shape, dtype, name):
+            return work.tile(shape, dtype, name=name, tag="stage", bufs=STAGE_BUFS, align_bytes=64)
+
+        def side_tile(shape, dtype, name):
+            return work.tile(shape, dtype, name=name, tag="side", bufs=SIDE_BUFS, align_bytes=64)
+
+        def load_bytes(n):
+            t = stage_tile([P, 2, 4096], U8, "k1b")
+            src = k1_bytes[2 * n : 2 * n + 2].rearrange("j (p t) l -> p j (t l)", t=4)
+            if n == 0:
+                for tt in range(4):
+                    cols = slice(tt * 1024, (tt + 1) * 1024)
+                    nc.sync.dma_start(out=t[:, 0, cols], in_=src[:, 0, cols])
+                nc.sync.dma_start(out=t[:, 1, :], in_=src[:, 1, :])
+            else:
+                nc.sync.dma_start(out=t[:], in_=src)
+            return t
+
+        def widen(n, t_bytes):
+            for jj in range(2):
+                j = 2 * n + jj
+                dst = planes[j // 8]
+                col = (j % 8) * 1024
+                for t in range(4):
+                    g = j * 4 + t
+                    src = t_bytes[:, jj, t * 1024 : (t + 1) * 1024].bitcast(FP8)
+                    o = dst[:, t, col : col + 1024]
+                    if g % 3 == 2:
+                        nc.scalar.activation(out=o, in_=src, func=ACT.Copy, scale=sc[:, t : t + 1])
+                    else:
+                        nc.vector.tensor_scalar(
+                            out=o, in0=src, scalar1=sc[:, t : t + 1], scalar2=None, op0=ALU.mult
+                        )
+
+        kb = {}
+        for n in range(4):
+            kb[n] = load_bytes(n)
+        for n in range(4):
+            widen(n, kb[n])
+            if n == 0:
+                permute_bias()
+            kb[n + 4] = load_bytes(n + 4)
+
+        xh = []
+        for hh in range(2):
+            xt = side_tile([P, 4096], BF16, "xh")
+            nc.sync.dma_start(
+                out=xt[:], in_=x[:, hh * 2048 : (hh + 1) * 2048, :].rearrange("b n c -> b (n c)")
+            )
+            xh.append(xt)
+        for c in range(3):
+            load_bias(c)
+        for n in range(4, 8):
+            widen(n, kb[n])
+
+        def gather(hh):
+            hw = side_tile([P, 2048], F32, "hw")
+            src = xh[hh][:].bitcast(F32).rearrange("b (g rr bc w) -> b g bc rr w", g=2, rr=16, bc=4, w=16)
+            dst = hw[:].rearrange("b (g bc rr w) -> b g bc rr w", g=2, bc=4, rr=16, w=16)
+            for g in range(2):
+                nc.vector.tensor_copy(out=dst[:, g], in_=src[:, g])
+            return hw
+
+        def turn(hw):
+            hg = side_tile([P, 4096], BF16, "hg")
+            hgw = hg[:].bitcast(F32).rearrange("p (jl b u) -> p jl b u", jl=8, b=128, u=2)
+            for pair in range(4):
+                pt = psum.tile([P, 4, 128], F32, name="pt", tag="bank")
+                for s in range(4):
+                    jl = pair * 2 + s // 2
+                    nc.tensor.transpose(
+                        out=pt[:, s, :], in_=hw[:, jl * 256 + s % 2 : (jl + 1) * 256 : 2], identity=ident[:]
+                    )
+                nc.scalar.copy(
+                    out=hgw[:, 2 * pair : 2 * pair + 2],
+                    in_=pt[:].rearrange("p (jl u) b -> p jl b u", u=2),
+                )
+            return hg
+
+        def quantize_h(hh, hg):
+            cols = slice(hh * 1024, (hh + 1) * 1024)
+            nc.vector.quantize_mx(out=hcodes[:, cols].bitcast(FP8X4), scales=hscl[:, cols], in_=hg[:])
+
+        grouped = {}
+        codes = {}
+        scl = {}
+        banks = {}
+        osb = {}
+
+        def interleave(u):
+            c, half = divmod(u, 2)
+            g = stage_tile([P, 4096], BF16, "grouped")
+            src = planes[half][:].rearrange("p t (n c i) -> p c n t i", c=NCHUNK, i=4)[:, c]
+            dst = g[:].rearrange("p (n i t) -> p n t i", i=4, t=4)
+            qv = 32 * VJ[u]
+            qg = qv + 32 * GJ[u]
+            if qv > 0:
+                nc.vector.tensor_copy(out=dst[:, :qv], in_=src[:, :qv])
+            if qg > qv:
+                nc.gpsimd.tensor_scalar(
+                    out=g[:].rearrange("p (n i t) -> p n i t", i=4, t=4)[:, qv:qg],
+                    in0=planes[half][:].rearrange("p t (n c i) -> p c n i t", c=NCHUNK, i=4)[:, c, qv:qg],
+                    scalar1=1.0,
+                    scalar2=0.0,
+                    op0=ALU.mult,
+                    op1=ALU.add,
+                )
+            nc.scalar.copy(out=dst[:, qg:], in_=src[:, qg:])
+            grouped[u] = g
+
+        def quantize(u):
+            cd = work.tile([P, 1024], U32, name="codes", tag="codes", bufs=2, align_bytes=64)
+            sl = work.tile([P, 1024], U8, name="scl", tag="scl", bufs=2, align_bytes=64)
+            nc.vector.quantize_mx(out=cd[:].bitcast(FP8X4), scales=sl[:], in_=grouped[u][:])
+            codes[u] = cd
+            scl[u] = sl
+
+        def multiply(u):
+            half = u % 2
+            tiles = []
+            for k in range(2):
+                ps = psum.tile([P, 512], F32, name="ps", tag="bank")
+                for jq in range(4):
+                    jl = k * 4 + jq
+                    j = half * 8 + jl
+                    nc.tensor.matmul_mx(
+                        out=ps[:, jq * 128 : (jq + 1) * 128],
+                        lhsT=hcodes[:, j * 128 : (j + 1) * 128].bitcast(FP8X4),
+                        lhsT_scale=hscl[:, j * 128 : (j + 1) * 128],
+                        rhs=codes[u][:, jl * 128 : (jl + 1) * 128].bitcast(FP8X4),
+                        rhs_scale=scl[u][:, jl * 128 : (jl + 1) * 128],
+                        start=True,
+                        stop=True,
+                    )
+                tiles.append(ps)
+            banks[u] = tiles
+
+        def add_bias(u):
+            c, half = divmod(u, 2)
+            if half == 0:
+                osb[c] = side_tile([P, 2048], F32, "osb")
+            ov = osb[c][:].rearrange("b (r q) -> b r q", q=128)
+            bv = bias_c[c][:].rearrange("b (r q) -> b r q", q=128)
+            parts = 2 if u == NUNIT - 1 else 1
+            rows = RC // parts
+            for part in range(parts):
+                rs = slice(part * rows, (part + 1) * rows)
+                for k in range(2):
+                    q0 = half * 64 + k * 32
+                    nc.vector.tensor_tensor(
+                        out=ov[:, rs, q0 : q0 + 32],
+                        in0=banks[u][k][:].rearrange("b (q r) -> b r q", r=RC)[:, rs, :],
+                        in1=bv[:, rs, q0 : q0 + 32],
+                        op=ALU.add,
+                    )
+                if half == 1:
+                    hs = slice(part * (4 // parts), (part + 1) * (4 // parts))
+                    nc.sync.dma_start(
+                        out=out.rearrange("b (rh c i) q -> c b rh (i q)", c=NCHUNK, i=4)[c][:, hs, :],
+                        in_=osb[c][:].rearrange("b (rh x) -> b rh x", rh=4)[:, hs, :],
+                    )
+            if half == 1 and c + 3 < NCHUNK:
+                load_bias(c + 3)
+
+        hw0 = gather(0)
+        hw1 = gather(1)
+        interleave(0)
+        hg0 = turn(hw0)
+        interleave(1)
+        hg1 = turn(hw1)
+        quantize(0)
+        quantize_h(0, hg0)
+        multiply(0)
+        for s in range(NUNIT):
+            if s + 2 < NUNIT:
+                interleave(s + 2)
+            if s == 0:
+                quantize_h(1, hg1)
+            if s + 1 < NUNIT:
+                quantize(s + 1)
+                multiply(s + 1)
+            add_bias(s)

@@ -23,6 +23,7 @@ STAGE_BUFS = 4
 SIDE_BUFS = 4
 VJ = [4, 4, 3, 3, 2, 2, 2, 2, 2, 2, 2, 2, 2, 2, 1, 1]
 GJ = [0, 0, 0, 0, 1, 1, 1, 1, 1, 1, 1, 1, 1, 1, 1, 1]
+TJ = [1, 1, 1, 1, 1, 1, 1, 1, 1, 1, 1, 1, 0, 0, 0, 0]
 
 
 def tile_switchnet_fstar_pa_kernel(tc, x, k1_bytes, k1_scale, b1, out):
@@ -42,6 +43,7 @@ def tile_switchnet_fstar_pa_kernel(tc, x, k1_bytes, k1_scale, b1, out):
         hcodes = keep.tile([P, 2048], U32, name="hcodes", align_bytes=64)
         hscl = keep.tile([P, 2048], U8, name="hscl", align_bytes=64)
         ident = keep.tile([P, P], F32, name="ident")
+        ident_bf = keep.tile([P, P], BF16, name="ident_bf")
         sc = keep.tile([P, 4], F32, name="sc")
         warm = keep.tile([P, 2], F32, name="warm")
 
@@ -50,6 +52,7 @@ def tile_switchnet_fstar_pa_kernel(tc, x, k1_bytes, k1_scale, b1, out):
         nc.vector.memset(warm[:], 0.0)
         nc.scalar.activation(out=warm[:, 1:2], in_=warm[:, 0:1], func=ACT.Copy)
         masks.make_identity(nc, ident[:])
+        masks.make_identity(nc, ident_bf[:])
 
         scratch = out[127].rearrange("r q -> (r q)").bitcast(BF16)[0:16384]
 
@@ -82,26 +85,26 @@ def tile_switchnet_fstar_pa_kernel(tc, x, k1_bytes, k1_scale, b1, out):
             return work.tile(shape, dtype, name=name, tag="side", bufs=SIDE_BUFS, align_bytes=64)
 
         def load_bytes(n):
-            t = stage_tile([P, 2, 4096], U8, "k1b")
-            src = k1_bytes[2 * n : 2 * n + 2].rearrange("j (p t) l -> p j (t l)", t=4)
-            if n == 0:
-                for tt in range(4):
-                    cols = slice(tt * 1024, (tt + 1) * 1024)
-                    nc.sync.dma_start(out=t[:, 0, cols], in_=src[:, 0, cols])
-                nc.sync.dma_start(out=t[:, 1, :], in_=src[:, 1, :])
-            else:
-                nc.sync.dma_start(out=t[:], in_=src)
+            t = stage_tile([P, 4, 2, 1024], U8, "k1b")
+            for jj in range(2):
+                src = k1_bytes[2 * n + jj].rearrange("(p t) l -> p t l", t=4)
+                if n == 0 and jj == 0:
+                    for tt in range(4):
+                        nc.sync.dma_start(out=t[:, tt, jj, :], in_=src[:, tt, :])
+                else:
+                    nc.sync.dma_start(out=t[:, :, jj, :], in_=src)
             return t
 
         def widen(n, t_bytes):
-            for jj in range(2):
-                j = 2 * n + jj
-                dst = planes[j // 8]
-                col = (j % 8) * 1024
+            dst = planes[n // 4]
+            col = (n % 4) * 2048
+            parts = 2 if n == 0 else 1
+            width = 2048 // parts
+            for part in range(parts):
                 for t in range(4):
-                    g = j * 4 + t
-                    src = t_bytes[:, jj, t * 1024 : (t + 1) * 1024].bitcast(FP8)
-                    o = dst[:, t, col : col + 1024]
+                    g = (n * parts + part) * 4 + t
+                    src = t_bytes[:, t].rearrange("p jj l -> p (jj l)")[:, part * width : (part + 1) * width].bitcast(FP8)
+                    o = dst[:, t, col + part * width : col + (part + 1) * width]
                     if g % 3 == 2:
                         nc.scalar.activation(out=o, in_=src, func=ACT.Copy, scale=sc[:, t : t + 1])
                     else:
@@ -171,6 +174,16 @@ def tile_switchnet_fstar_pa_kernel(tc, x, k1_bytes, k1_scale, b1, out):
             dst = g[:].rearrange("p (n i t) -> p n t i", i=4, t=4)
             qv = 32 * VJ[u]
             qg = qv + 32 * GJ[u]
+            qs = 256 - 32 * TJ[u]
+            if qs < 256:
+                pp = psum.tile([P, 512], BF16, name="pp", tag="bank")
+                nc.tensor.matmul(
+                    out=pp[:].rearrange("p (n i t) -> p n i t", i=4, t=4),
+                    lhsT=ident_bf[:],
+                    rhs=planes[half][:].rearrange("p t (n c i) -> p c n i t", c=NCHUNK, i=4)[:, c, qs:],
+                    start=True,
+                    stop=True,
+                )
             if qv > 0:
                 nc.vector.tensor_copy(out=dst[:, :qv], in_=src[:, :qv])
             if qg > qv:
@@ -182,7 +195,9 @@ def tile_switchnet_fstar_pa_kernel(tc, x, k1_bytes, k1_scale, b1, out):
                     op0=ALU.mult,
                     op1=ALU.add,
                 )
-            nc.scalar.copy(out=dst[:, qg:], in_=src[:, qg:])
+            nc.scalar.copy(out=dst[:, qg:qs], in_=src[:, qg:qs])
+            if qs < 256:
+                nc.scalar.copy(out=g[:, 16 * qs :], in_=pp[:])
             grouped[u] = g
 
         def quantize(u):

@@ -21,7 +21,7 @@ NCHUNK = 128 // RC
 NUNIT = 2 * NCHUNK
 STAGE_BUFS = 4
 SIDE_BUFS = 4
-VJ = [4, 4, 3, 3, 2, 2, 2, 2, 2, 2, 2, 2, 2, 2, 1, 1]
+VJ = [4, 4, 3, 3, 2, 1, 2, 1, 2, 1, 2, 1, 2, 2, 1, 1]
 GJ = [0, 0, 0, 0, 1, 1, 1, 1, 1, 1, 1, 1, 1, 1, 1, 1]
 TJ = [1, 1, 1, 1, 1, 1, 1, 1, 1, 1, 1, 1, 0, 0, 0, 0]
 

@@ -17,6 +17,9 @@ ALU = mybir.AluOpType
 P = 128
 NJ = 16
 RC = 16
+IR = 8
+NRH = RC // IR
+NJN = 128 // IR
 NCHUNK = 128 // RC
 NUNIT = 2 * NCHUNK
 STAGE_BUFS = 4
@@ -57,12 +60,10 @@ def tile_switchnet_fstar_pa_kernel(tc, x, k1_bytes, k1_scale, b1, out):
         scratch = out[127].rearrange("r q -> (r q)").bitcast(BF16)[0:16384]
 
         def permute_bias():
-            for h in range(2):
-                cols = slice(h * 64, (h + 1) * 64)
-                nc.vector.tensor_copy(
-                    out=b_f32[:, cols].rearrange("q (c e i) -> q c e i", c=8, e=2, i=4),
-                    in_=b_nat[:, cols].rearrange("q (e c i) -> q c e i", e=2, c=8, i=4),
-                )
+            nc.vector.tensor_copy(
+                out=b_f32[:].rearrange("q (c rh i) -> q c rh i", c=NCHUNK, rh=NRH, i=IR),
+                in_=b_nat[:].rearrange("q (rh c i) -> q c rh i", rh=NRH, c=NCHUNK, i=IR),
+            )
             pb = psum.tile([P, 4, 128], F32, name="pb", tag="bank")
             nc.tensor.transpose(out=pb[:, 0, :], in_=b_f32[:], identity=ident[:])
             nc.scalar.copy(out=b_t[:], in_=pb[:, 0, :])
@@ -72,10 +73,7 @@ def tile_switchnet_fstar_pa_kernel(tc, x, k1_bytes, k1_scale, b1, out):
 
         def load_bias(c):
             bt = work.tile([P, 2048], BF16, name="bias_c", tag="bias_c", bufs=3, align_bytes=64)
-            nc.sync.dma_start(
-                out=bt[:].rearrange("b (h x) -> b h x", h=2),
-                in_=scratch.rearrange("(h c x) -> c h x", h=2, c=NCHUNK)[c].partition_broadcast(P),
-            )
+            nc.sync.dma_start(out=bt[:], in_=scratch.rearrange("(c x) -> c x", c=NCHUNK)[c].partition_broadcast(P))
             bias_c[c] = bt
 
         def stage_tile(shape, dtype, name):
@@ -170,17 +168,17 @@ def tile_switchnet_fstar_pa_kernel(tc, x, k1_bytes, k1_scale, b1, out):
         def interleave(u):
             c, half = divmod(u, 2)
             g = stage_tile([P, 4096], BF16, "grouped")
-            src = planes[half][:].rearrange("p t (n c i) -> p c n t i", c=NCHUNK, i=4)[:, c]
-            dst = g[:].rearrange("p (n i t) -> p n t i", i=4, t=4)
-            qv = 32 * VJ[u]
-            qg = qv + 32 * GJ[u]
-            qs = 256 - 32 * TJ[u]
-            if qs < 256:
+            src = planes[half][:].rearrange("p t (n c i) -> p c n t i", c=NCHUNK, i=IR)[:, c]
+            dst = g[:].rearrange("p (n i t) -> p n t i", i=IR, t=4)
+            qv = NJN * VJ[u]
+            qg = qv + NJN * GJ[u]
+            qs = NJN * (8 - TJ[u])
+            if TJ[u] > 0:
                 pp = psum.tile([P, 512], BF16, name="pp", tag="bank")
                 nc.tensor.matmul(
-                    out=pp[:].rearrange("p (n i t) -> p n i t", i=4, t=4),
+                    out=pp[:].rearrange("p (n i t) -> p n i t", i=IR, t=4),
                     lhsT=ident_bf[:],
-                    rhs=planes[half][:].rearrange("p t (n c i) -> p c n i t", c=NCHUNK, i=4)[:, c, qs:],
+                    rhs=planes[half][:].rearrange("p t (n c i) -> p c n i t", c=NCHUNK, i=IR)[:, c, qs:],
                     start=True,
                     stop=True,
                 )
@@ -188,16 +186,16 @@ def tile_switchnet_fstar_pa_kernel(tc, x, k1_bytes, k1_scale, b1, out):
                 nc.vector.tensor_copy(out=dst[:, :qv], in_=src[:, :qv])
             if qg > qv:
                 nc.gpsimd.tensor_scalar(
-                    out=g[:].rearrange("p (n i t) -> p n i t", i=4, t=4)[:, qv:qg],
-                    in0=planes[half][:].rearrange("p t (n c i) -> p c n i t", c=NCHUNK, i=4)[:, c, qv:qg],
+                    out=g[:].rearrange("p (n i t) -> p n i t", i=IR, t=4)[:, qv:qg],
+                    in0=planes[half][:].rearrange("p t (n c i) -> p c n i t", c=NCHUNK, i=IR)[:, c, qv:qg],
                     scalar1=1.0,
                     scalar2=0.0,
                     op0=ALU.mult,
                     op1=ALU.add,
                 )
             nc.scalar.copy(out=dst[:, qg:qs], in_=src[:, qg:qs])
-            if qs < 256:
-                nc.scalar.copy(out=g[:, 16 * qs :], in_=pp[:])
+            if TJ[u] > 0:
+                nc.scalar.copy(out=g[:, 4 * IR * qs :], in_=pp[:])
             grouped[u] = g
 
         def quantize(u):
@@ -246,10 +244,10 @@ def tile_switchnet_fstar_pa_kernel(tc, x, k1_bytes, k1_scale, b1, out):
                         op=ALU.add,
                     )
                 if half == 1:
-                    hs = slice(part * (4 // parts), (part + 1) * (4 // parts))
+                    hs = slice(part * (NRH // parts), (part + 1) * (NRH // parts))
                     nc.sync.dma_start(
-                        out=out.rearrange("b (rh c i) q -> c b rh (i q)", c=NCHUNK, i=4)[c][:, hs, :],
-                        in_=osb[c][:].rearrange("b (rh x) -> b rh x", rh=4)[:, hs, :],
+                        out=out.rearrange("b (rh c i) q -> c b rh (i q)", c=NCHUNK, i=IR)[c][:, hs, :],
+                        in_=osb[c][:].rearrange("b (rh x) -> b rh x", rh=NRH)[:, hs, :],
                     )
             if half == 1 and c + 3 < NCHUNK:
                 load_bias(c + 3)

@@ -22,9 +22,11 @@ NRH = RC // IR
 NJN = 128 // IR
 NCHUNK = 128 // RC
 NUNIT = 2 * NCHUNK
+LAST = NUNIT - 1
+LAST_ROWS = [(0, 8), (8, 12), (12, 14), (14, 16)]
 STAGE_BUFS = 4
 SIDE_BUFS = 4
-VJ = [4, 4, 3, 3, 2, 1, 2, 1, 2, 1, 2, 1, 2, 2, 1, 1]
+VJ = [4, 4, 3, 3, 2, 1, 2, 1, 2, 1, 1, 1, 2, 2, 1, 1]
 GJ = [0, 0, 0, 0, 1, 1, 1, 1, 1, 1, 1, 1, 1, 1, 1, 1]
 TJ = [1, 1, 1, 1, 1, 1, 1, 1, 1, 1, 1, 1, 0, 0, 0, 0]
 
@@ -198,17 +200,66 @@ def tile_switchnet_fstar_pa_kernel(tc, x, k1_bytes, k1_scale, b1, out):
                 nc.scalar.copy(out=g[:, 4 * IR * qs :], in_=pp[:])
             grouped[u] = g
 
-        def quantize(u):
-            cd = work.tile([P, 1024], U32, name="codes", tag="codes", bufs=2, align_bytes=64)
-            sl = work.tile([P, 1024], U8, name="scl", tag="scl", bufs=2, align_bytes=64)
-            nc.vector.quantize_mx(out=cd[:].bitcast(FP8X4), scales=sl[:], in_=grouped[u][:])
-            codes[u] = cd
-            scl[u] = sl
+        def interleave_last():
+            c, half = divmod(LAST, 2)
+            g = stage_tile([P, 4096], BF16, "grouped")
+            mv = 8 * VJ[LAST]
+            mg = mv + 8 * GJ[LAST]
+            for rh in range(NRH):
+                src = planes[half][:].rearrange("p t (n rh c i) -> p c rh n t i", rh=NRH, c=NCHUNK, i=IR)[:, c, rh]
+                dst = g[:].rearrange("p (rh n i t) -> p rh n t i", rh=NRH, i=IR, t=4)[:, rh]
+                nc.vector.tensor_copy(out=dst[:, :mv], in_=src[:, :mv])
+                nc.gpsimd.tensor_scalar(
+                    out=g[:].rearrange("p (rh n i t) -> p rh n i t", rh=NRH, i=IR, t=4)[:, rh, mv:mg],
+                    in0=planes[half][:].rearrange("p t (n rh c i) -> p c rh n i t", rh=NRH, c=NCHUNK, i=IR)[:, c, rh, mv:mg],
+                    scalar1=1.0,
+                    scalar2=0.0,
+                    op0=ALU.mult,
+                    op1=ALU.add,
+                )
+                nc.scalar.copy(out=dst[:, mg:], in_=src[:, mg:])
+            grouped[LAST] = g
 
-        def multiply(u):
+        def multiply_last(rh):
+            ps = psum.tile([P, 512], F32, name="ps", tag="bank")
+            for jl in range(8):
+                j = 8 + jl
+                cols = slice(rh * 512 + jl * 64, rh * 512 + (jl + 1) * 64)
+                nc.tensor.matmul_mx(
+                    out=ps[:, jl * 64 : (jl + 1) * 64],
+                    lhsT=hcodes[:, j * 128 : (j + 1) * 128].bitcast(FP8X4),
+                    lhsT_scale=hscl[:, j * 128 : (j + 1) * 128],
+                    rhs=codes[LAST][:, cols].bitcast(FP8X4),
+                    rhs_scale=scl[LAST][:, cols],
+                    start=True,
+                    stop=True,
+                )
+            banks[(LAST, rh)] = ps
+
+        def add_rows_last(r0, r1):
+            c = NCHUNK - 1
+            rh = r0 // IR
+            nc.vector.tensor_tensor(
+                out=osb[c][:].rearrange("b (r q) -> b r q", q=128)[:, r0:r1, 64:128],
+                in0=banks[(LAST, rh)][:].rearrange("b (q i) -> b i q", i=IR)[:, r0 - rh * IR : r1 - rh * IR, :],
+                in1=bias_c[c][:].rearrange("b (r q) -> b r q", q=128)[:, r0:r1, 64:128],
+                op=ALU.add,
+            )
+
+        def quantize(u, ks=(0, 1)):
+            if ks[0] == 0:
+                codes[u] = work.tile([P, 1024], U32, name="codes", tag="codes", bufs=2, align_bytes=64)
+                scl[u] = work.tile([P, 1024], U8, name="scl", tag="scl", bufs=2, align_bytes=64)
+            cols = slice(ks[0] * 512, (ks[-1] + 1) * 512)
+            nc.vector.quantize_mx(
+                out=codes[u][:, cols].bitcast(FP8X4),
+                scales=scl[u][:, cols],
+                in_=grouped[u][:, 4 * cols.start : 4 * cols.stop],
+            )
+
+        def multiply(u, ks=(0, 1)):
             half = u % 2
-            tiles = []
-            for k in range(2):
+            for k in ks:
                 ps = psum.tile([P, 512], F32, name="ps", tag="bank")
                 for jq in range(4):
                     jl = k * 4 + jq
@@ -222,35 +273,38 @@ def tile_switchnet_fstar_pa_kernel(tc, x, k1_bytes, k1_scale, b1, out):
                         start=True,
                         stop=True,
                     )
-                tiles.append(ps)
-            banks[u] = tiles
+                banks[(u, k)] = ps
+
+        def add_rows(u, k, r0, r1):
+            c, half = divmod(u, 2)
+            q0 = half * 64 + k * 32
+            nc.vector.tensor_tensor(
+                out=osb[c][:].rearrange("b (r q) -> b r q", q=128)[:, r0:r1, q0 : q0 + 32],
+                in0=banks[(u, k)][:].rearrange("b (q r) -> b r q", r=RC)[:, r0:r1, :],
+                in1=bias_c[c][:].rearrange("b (r q) -> b r q", q=128)[:, r0:r1, q0 : q0 + 32],
+                op=ALU.add,
+            )
+
+        def store_rows(c, r0, r1):
+            dst = out.rearrange("b (rh c i) q -> c b rh (i q)", c=NCHUNK, i=IR)[c]
+            if r1 - r0 == RC:
+                nc.sync.dma_start(out=dst, in_=osb[c][:].rearrange("b (rh x) -> b rh x", rh=NRH))
+            else:
+                rh = r0 // IR
+                nc.sync.dma_start(
+                    out=dst[:, rh, (r0 - rh * IR) * 128 : (r1 - rh * IR) * 128], in_=osb[c][:, r0 * 128 : r1 * 128]
+                )
 
         def add_bias(u):
             c, half = divmod(u, 2)
             if half == 0:
                 osb[c] = side_tile([P, 2048], F32, "osb")
-            ov = osb[c][:].rearrange("b (r q) -> b r q", q=128)
-            bv = bias_c[c][:].rearrange("b (r q) -> b r q", q=128)
-            parts = 2 if u == NUNIT - 1 else 1
-            rows = RC // parts
-            for part in range(parts):
-                rs = slice(part * rows, (part + 1) * rows)
-                for k in range(2):
-                    q0 = half * 64 + k * 32
-                    nc.vector.tensor_tensor(
-                        out=ov[:, rs, q0 : q0 + 32],
-                        in0=banks[u][k][:].rearrange("b (q r) -> b r q", r=RC)[:, rs, :],
-                        in1=bv[:, rs, q0 : q0 + 32],
-                        op=ALU.add,
-                    )
-                if half == 1:
-                    hs = slice(part * (NRH // parts), (part + 1) * (NRH // parts))
-                    nc.sync.dma_start(
-                        out=out.rearrange("b (rh c i) q -> c b rh (i q)", c=NCHUNK, i=IR)[c][:, hs, :],
-                        in_=osb[c][:].rearrange("b (rh x) -> b rh x", rh=NRH)[:, hs, :],
-                    )
-            if half == 1 and c + 3 < NCHUNK:
-                load_bias(c + 3)
+            for k in range(2):
+                add_rows(u, k, 0, RC)
+            if half == 1:
+                store_rows(c, 0, RC)
+                if c + 3 < NCHUNK:
+                    load_bias(c + 3)
 
         hw0 = gather(0)
         hw1 = gather(1)
@@ -261,12 +315,20 @@ def tile_switchnet_fstar_pa_kernel(tc, x, k1_bytes, k1_scale, b1, out):
         quantize(0)
         quantize_h(0, hg0)
         multiply(0)
-        for s in range(NUNIT):
-            if s + 2 < NUNIT:
+        for s in range(LAST - 1):
+            if s + 2 < LAST:
                 interleave(s + 2)
+            else:
+                interleave_last()
             if s == 0:
                 quantize_h(1, hg1)
-            if s + 1 < NUNIT:
-                quantize(s + 1)
-                multiply(s + 1)
+            quantize(s + 1)
+            multiply(s + 1)
             add_bias(s)
+        for rh in range(NRH):
+            quantize(LAST, (rh,))
+            multiply_last(rh)
+        add_bias(LAST - 1)
+        for r0, r1 in LAST_ROWS:
+            add_rows_last(r0, r1)
+            store_rows(NCHUNK - 1, r0, r1)

@@ -188,8 +188,8 @@ def tile_switchnet_fstar_pa_kernel(tc, x, k1_bytes, k1_scale, b1, out):
                 nc.vector.tensor_copy(out=dst[:, :qv], in_=src[:, :qv])
             if qg > qv:
                 nc.gpsimd.tensor_scalar(
-                    out=g[:].rearrange("p (n i t) -> p n i t", i=IR, t=4)[:, qv:qg],
-                    in0=planes[half][:].rearrange("p t (n c i) -> p c n i t", c=NCHUNK, i=IR)[:, c, qv:qg],
+                    out=dst[:, qv:qg],
+                    in0=src[:, qv:qg],
                     scalar1=1.0,
                     scalar2=0.0,
                     op0=ALU.mult,
@@ -210,8 +210,8 @@ def tile_switchnet_fstar_pa_kernel(tc, x, k1_bytes, k1_scale, b1, out):
                 dst = g[:].rearrange("p (rh n i t) -> p rh n t i", rh=NRH, i=IR, t=4)[:, rh]
                 nc.vector.tensor_copy(out=dst[:, :mv], in_=src[:, :mv])
                 nc.gpsimd.tensor_scalar(
-                    out=g[:].rearrange("p (rh n i t) -> p rh n i t", rh=NRH, i=IR, t=4)[:, rh, mv:mg],
-                    in0=planes[half][:].rearrange("p t (n rh c i) -> p c rh n i t", rh=NRH, c=NCHUNK, i=IR)[:, c, rh, mv:mg],
+                    out=dst[:, mv:mg],
+                    in0=src[:, mv:mg],
                     scalar1=1.0,
                     scalar2=0.0,
                     op0=ALU.mult,

@@ -26,8 +26,8 @@ LAST = NUNIT - 1
 LAST_ROWS = [(0, 8), (8, 12), (12, 14), (14, 16)]
 STAGE_BUFS = 4
 SIDE_BUFS = 4
-VJ = [4, 4, 3, 3, 2, 1, 2, 1, 2, 1, 1, 1, 2, 2, 1, 1]
-GJ = [0, 0, 0, 0, 1, 1, 1, 1, 1, 1, 1, 1, 1, 1, 1, 1]
+VJ = [4, 4, 3, 3, 1, 1, 2, 1, 1, 1, 1, 1, 2, 2, 1, 1]
+GQ = [0, 0, 0, 0, 5, 5, 5, 5, 5, 5, 5, 5, 5, 5, 5, 5]
 TJ = [1, 1, 1, 1, 1, 1, 1, 1, 1, 1, 1, 1, 0, 0, 0, 0]
 
 
@@ -173,7 +173,7 @@ def tile_switchnet_fstar_pa_kernel(tc, x, k1_bytes, k1_scale, b1, out):
             src = planes[half][:].rearrange("p t (n c i) -> p c n t i", c=NCHUNK, i=IR)[:, c]
             dst = g[:].rearrange("p (n i t) -> p n t i", i=IR, t=4)
             qv = NJN * VJ[u]
-            qg = qv + NJN * GJ[u]
+            qg = qv + (NJN // 4) * GQ[u]
             qs = NJN * (8 - TJ[u])
             if TJ[u] > 0:
                 pp = psum.tile([P, 512], BF16, name="pp", tag="bank")
@@ -204,7 +204,7 @@ def tile_switchnet_fstar_pa_kernel(tc, x, k1_bytes, k1_scale, b1, out):
             c, half = divmod(LAST, 2)
             g = stage_tile([P, 4096], BF16, "grouped")
             mv = 8 * VJ[LAST]
-            mg = mv + 8 * GJ[LAST]
+            mg = mv + 2 * GQ[LAST]
             for rh in range(NRH):
                 src = planes[half][:].rearrange("p t (n rh c i) -> p c rh n t i", rh=NRH, c=NCHUNK, i=IR)[:, c, rh]
                 dst = g[:].rearrange("p (rh n i t) -> p rh n t i", rh=NRH, i=IR, t=4)[:, rh]

@@ -15,20 +15,19 @@ ACT = mybir.ActivationFunctionType
 ALU = mybir.AluOpType
 
 P = 128
-NJ = 16
 RC = 16
 IR = 8
 NRH = RC // IR
-NJN = 128 // IR
 NCHUNK = 128 // RC
-NUNIT = 2 * NCHUNK
-LAST = NUNIT - 1
+NJN = 128 // IR
+LASTC = NCHUNK - 1
 LAST_ROWS = [(0, 8), (8, 12), (12, 14), (14, 16)]
-STAGE_BUFS = 4
-SIDE_BUFS = 4
-VJ = [4, 4, 3, 3, 1, 1, 2, 1, 1, 1, 1, 1, 2, 2, 1, 1]
-GQ = [0, 0, 0, 0, 5, 5, 5, 5, 5, 5, 5, 5, 5, 5, 5, 5]
-TJ = [1, 1, 1, 1, 1, 1, 1, 1, 1, 1, 1, 1, 0, 0, 0, 0]
+S_WIDEN = {("E0", 0, 2), ("E0", 1, 1), ("E0", 1, 3), ("L1", 0, 3), ("L2", 0, 3)}
+SPLIT = {"E0"}
+T_BLOCKS = {(0, 7), (1, 7), (2, 7), (3, 7), (1, 6), (3, 6)}
+V_BLOCKS = {(9, 9)}
+G_RUNS = [0, 0, 48, 48, 48, 48, 48, 48]
+V_RUNS = [0, 24, 0, 0, 0, 0, 0, 0]
 
 
 def tile_switchnet_fstar_pa_kernel(tc, x, k1_bytes, k1_scale, b1, out):
@@ -39,9 +38,9 @@ def tile_switchnet_fstar_pa_kernel(tc, x, k1_bytes, k1_scale, b1, out):
         psum = ctx.enter_context(tc.psum_pool(name="psum", bufs=8))
         ctx.enter_context(tc.manual_schedule())
 
-        planes_a = keep.tile([P, 4, 8192], BF16, name="planes_a")
-        planes_b = keep.tile([P, 4, 8192], BF16, name="planes_b")
-        planes = [planes_a, planes_b]
+        planes = keep.tile([P, 4, 8192], BF16, name="planes")
+        codes0 = keep.tile([P, 8192], U32, name="codes0", align_bytes=64)
+        scl0 = keep.tile([P, 8192], U8, name="scl0", align_bytes=64)
         b_nat = keep.tile([P, P], BF16, name="b_nat")
         b_f32 = keep.tile([P, P], F32, name="b_f32")
         b_t = keep.tile([P, P], BF16, name="b_t")
@@ -73,65 +72,105 @@ def tile_switchnet_fstar_pa_kernel(tc, x, k1_bytes, k1_scale, b1, out):
 
         bias_c = {}
 
-        def load_bias(c):
-            bt = work.tile([P, 2048], BF16, name="bias_c", tag="bias_c", bufs=3, align_bytes=64)
-            nc.sync.dma_start(out=bt[:], in_=scratch.rearrange("(c x) -> c x", c=NCHUNK)[c].partition_broadcast(P))
-            bias_c[c] = bt
-
-        def stage_tile(shape, dtype, name):
-            return work.tile(shape, dtype, name=name, tag="stage", bufs=STAGE_BUFS, align_bytes=64)
+        def load_bias(b):
+            if b == 0:
+                bt = keep.tile([P, 4096], BF16, name="bias_0", align_bytes=64)
+            else:
+                bt = work.tile([P, 4096], BF16, name="bias_c", tag="bytes", bufs=3, align_bytes=64)
+            nc.sync.dma_start(out=bt[:], in_=scratch.rearrange("(b x) -> b x", b=NCHUNK // 2)[b].partition_broadcast(P))
+            for e in range(2):
+                bias_c[2 * b + e] = bt[:, e * 2048 : (e + 1) * 2048]
 
         def side_tile(shape, dtype, name):
-            return work.tile(shape, dtype, name=name, tag="side", bufs=SIDE_BUFS, align_bytes=64)
+            return work.tile(shape, dtype, name=name, tag="side", bufs=3, align_bytes=64)
 
-        def load_bytes(n):
-            t = stage_tile([P, 4, 2, 1024], U8, "k1b")
+        def pair_tile(shape, name):
+            return work.tile(shape, BF16, name=name, tag="pair", bufs=2, align_bytes=64)
+
+        kb = {}
+        early = {}
+
+        def load_bytes(name):
+            n = int(name[1:])
+            j0 = 2 * n if name[0] == "E" else 8 + 2 * n
+            t = work.tile([P, 4, 2, 1024], U8, name="k1b", tag="bytes", bufs=3, align_bytes=64)
             for jj in range(2):
-                src = k1_bytes[2 * n + jj].rearrange("(p t) l -> p t l", t=4)
-                if n == 0 and jj == 0:
+                src = k1_bytes[j0 + jj].rearrange("(p t) l -> p t l", t=4)
+                if name == "E0" and jj == 0:
                     for tt in range(4):
                         nc.sync.dma_start(out=t[:, tt, jj, :], in_=src[:, tt, :])
+                elif name == "E0":
+                    for tt in range(0, 4, 2):
+                        nc.sync.dma_start(out=t[:, tt : tt + 2, jj, :], in_=src[:, tt : tt + 2, :])
+                elif name == "E1":
+                    if jj == 0:
+                        both = k1_bytes[j0 : j0 + 2].rearrange("jj (p t) l -> p t jj l", t=4)
+                        for tt in range(4):
+                            nc.sync.dma_start(out=t[:, tt], in_=both[:, tt])
                 else:
                     nc.sync.dma_start(out=t[:, :, jj, :], in_=src)
-            return t
+            kb[name] = t
 
-        def widen(n, t_bytes):
-            dst = planes[n // 4]
-            col = (n % 4) * 2048
-            parts = 2 if n == 0 else 1
+        def widen(name):
+            n = int(name[1:])
+            if name[0] == "L":
+                dst = planes[:, :, n * 2048 : (n + 1) * 2048]
+            else:
+                early[n] = pair_tile([P, 4, 2048], "early")
+                dst = early[n][:]
+            parts = 2 if name in SPLIT else 1
             width = 2048 // parts
             for part in range(parts):
                 for t in range(4):
-                    g = (n * parts + part) * 4 + t
-                    src = t_bytes[:, t].rearrange("p jj l -> p (jj l)")[:, part * width : (part + 1) * width].bitcast(FP8)
-                    o = dst[:, t, col + part * width : col + (part + 1) * width]
-                    if g % 3 == 2:
+                    cols = slice(part * width, (part + 1) * width)
+                    src = kb[name][:, t].rearrange("p jj l -> p (jj l)")[:, cols].bitcast(FP8)
+                    o = dst[:, t, cols]
+                    if (name, part, t) in S_WIDEN:
                         nc.scalar.activation(out=o, in_=src, func=ACT.Copy, scale=sc[:, t : t + 1])
                     else:
                         nc.vector.tensor_scalar(
                             out=o, in0=src, scalar1=sc[:, t : t + 1], scalar2=None, op0=ALU.mult
                         )
 
-        kb = {}
-        for n in range(4):
-            kb[n] = load_bytes(n)
-        for n in range(4):
-            widen(n, kb[n])
-            if n == 0:
-                permute_bias()
-            kb[n + 4] = load_bytes(n + 4)
+        eg = {}
+
+        def early_interleave(n, g):
+            e = work.tile([P, 4096], BF16, name="eg", tag="eg", bufs=3, align_bytes=64)
+            view = early[n][:].rearrange("p t (n c i) -> p c n t i", c=NCHUNK, i=IR)
+            tview = early[n][:].rearrange("p t (n c i) -> p c n i t", c=NCHUNK, i=IR)
+            for cl in range(4):
+                c = 4 * g + cl
+                o = e[:, cl * 1024 : (cl + 1) * 1024]
+                if (n, c) in T_BLOCKS:
+                    pp = psum.tile([P, 1024], BF16, name="pp", tag="bank")
+                    for jj in range(2):
+                        nc.tensor.matmul(
+                            out=pp[:, jj * 512 : (jj + 1) * 512].rearrange("p (n i t) -> p n i t", i=IR, t=4),
+                            lhsT=ident_bf[:],
+                            rhs=tview[:, c, jj * NJN : (jj + 1) * NJN],
+                            start=True,
+                            stop=True,
+                        )
+                    nc.scalar.copy(out=o, in_=pp[:])
+                elif (n, c) in V_BLOCKS:
+                    nc.vector.tensor_copy(out=o.rearrange("p (n i t) -> p n t i", i=IR, t=4), in_=view[:, c])
+                else:
+                    nc.scalar.copy(out=o.rearrange("p (n i t) -> p n t i", i=IR, t=4), in_=view[:, c])
+            eg[(n, g)] = e
+
+        def early_quantize(n, g):
+            cols = slice(n * 2048 + g * 1024, n * 2048 + (g + 1) * 1024)
+            nc.vector.quantize_mx(out=codes0[:, cols].bitcast(FP8X4), scales=scl0[:, cols], in_=eg[(n, g)][:])
 
         xh = []
-        for hh in range(2):
-            xt = side_tile([P, 4096], BF16, "xh")
-            nc.sync.dma_start(
-                out=xt[:], in_=x[:, hh * 2048 : (hh + 1) * 2048, :].rearrange("b n c -> b (n c)")
-            )
-            xh.append(xt)
-        for c in range(3):
-            load_bias(c)
-        for n in range(4, 8):
-            widen(n, kb[n])
+
+        def load_x():
+            for hh in range(2):
+                xt = side_tile([P, 4096], BF16, "xh")
+                nc.sync.dma_start(
+                    out=xt[:], in_=x[:, hh * 2048 : (hh + 1) * 2048, :].rearrange("b n c -> b (n c)")
+                )
+                xh.append(xt)
 
         def gather(hh):
             hw = side_tile([P, 2048], F32, "hw")
@@ -161,127 +200,105 @@ def tile_switchnet_fstar_pa_kernel(tc, x, k1_bytes, k1_scale, b1, out):
             cols = slice(hh * 1024, (hh + 1) * 1024)
             nc.vector.quantize_mx(out=hcodes[:, cols].bitcast(FP8X4), scales=hscl[:, cols], in_=hg[:])
 
-        grouped = {}
+        lg = {}
         codes = {}
         scl = {}
         banks = {}
         osb = {}
 
-        def interleave(u):
-            c, half = divmod(u, 2)
-            g = stage_tile([P, 4096], BF16, "grouped")
-            src = planes[half][:].rearrange("p t (n c i) -> p c n t i", c=NCHUNK, i=IR)[:, c]
-            dst = g[:].rearrange("p (n i t) -> p n t i", i=IR, t=4)
-            qv = NJN * VJ[u]
-            qg = qv + (NJN // 4) * GQ[u]
-            qs = NJN * (8 - TJ[u])
-            if TJ[u] > 0:
-                pp = psum.tile([P, 512], BF16, name="pp", tag="bank")
-                nc.tensor.matmul(
-                    out=pp[:].rearrange("p (n i t) -> p n i t", i=IR, t=4),
-                    lhsT=ident_bf[:],
-                    rhs=planes[half][:].rearrange("p t (n c i) -> p c n i t", c=NCHUNK, i=IR)[:, c, qs:],
-                    start=True,
-                    stop=True,
-                )
-            if qv > 0:
-                nc.vector.tensor_copy(out=dst[:, :qv], in_=src[:, :qv])
-            if qg > qv:
+        def copy_runs(dst, src, g, v):
+            if g > 0:
                 nc.gpsimd.tensor_scalar(
-                    out=dst[:, qv:qg],
-                    in0=src[:, qv:qg],
-                    scalar1=1.0,
-                    scalar2=0.0,
-                    op0=ALU.mult,
-                    op1=ALU.add,
+                    out=dst[:, :g], in0=src[:, :g], scalar1=1.0, scalar2=0.0, op0=ALU.mult, op1=ALU.add
                 )
-            nc.scalar.copy(out=dst[:, qg:qs], in_=src[:, qg:qs])
-            if TJ[u] > 0:
-                nc.scalar.copy(out=g[:, 4 * IR * qs :], in_=pp[:])
-            grouped[u] = g
+            n = dst.shape[1]
+            nc.scalar.copy(out=dst[:, g : n - v], in_=src[:, g : n - v])
+            if v > 0:
+                nc.vector.tensor_copy(out=dst[:, n - v :], in_=src[:, n - v :])
 
-        def interleave_last():
-            c, half = divmod(LAST, 2)
-            g = stage_tile([P, 4096], BF16, "grouped")
-            mv = 8 * VJ[LAST]
-            mg = mv + 2 * GQ[LAST]
-            for rh in range(NRH):
-                src = planes[half][:].rearrange("p t (n rh c i) -> p c rh n t i", rh=NRH, c=NCHUNK, i=IR)[:, c, rh]
-                dst = g[:].rearrange("p (rh n i t) -> p rh n t i", rh=NRH, i=IR, t=4)[:, rh]
-                nc.vector.tensor_copy(out=dst[:, :mv], in_=src[:, :mv])
-                nc.gpsimd.tensor_scalar(
-                    out=dst[:, mv:mg],
-                    in0=src[:, mv:mg],
-                    scalar1=1.0,
-                    scalar2=0.0,
-                    op0=ALU.mult,
-                    op1=ALU.add,
+        late_buf = []
+
+        def late_interleave(c):
+            if not late_buf:
+                late_buf.append(pair_tile([P, 8192], "late_buf"))
+            t = late_buf[0][:, c % 2 * 4096 : (c % 2 + 1) * 4096]
+            if c < LASTC:
+                copy_runs(
+                    t.rearrange("p (n i t) -> p n t i", i=IR, t=4),
+                    planes[:].rearrange("p t (n c i) -> p c n t i", c=NCHUNK, i=IR)[:, c],
+                    G_RUNS[c],
+                    V_RUNS[c],
                 )
-                nc.scalar.copy(out=dst[:, mg:], in_=src[:, mg:])
-            grouped[LAST] = g
+            else:
+                for rh in range(NRH):
+                    copy_runs(
+                        t.rearrange("p (rh n i t) -> p rh n t i", rh=NRH, i=IR, t=4)[:, rh],
+                        planes[:].rearrange("p t (n rh c i) -> p c rh n t i", rh=NRH, c=NCHUNK, i=IR)[:, c, rh],
+                        G_RUNS[c] // NRH,
+                        V_RUNS[c] // NRH,
+                    )
+            lg[c] = t
+
+        def quantize(c, ks=(0, 1)):
+            if ks[0] == 0:
+                codes[c] = work.tile([P, 1024], U32, name="codes", tag="codes", bufs=2, align_bytes=64)
+                scl[c] = work.tile([P, 1024], U8, name="scl", tag="scl", bufs=2, align_bytes=64)
+            cols = slice(ks[0] * 512, (ks[-1] + 1) * 512)
+            nc.vector.quantize_mx(
+                out=codes[c][:, cols].bitcast(FP8X4),
+                scales=scl[c][:, cols],
+                in_=lg[c][:, 4 * cols.start : 4 * cols.stop],
+            )
+
+        def one_pass(out_ap, j, w, ws, cols):
+            nc.tensor.matmul_mx(
+                out=out_ap,
+                lhsT=hcodes[:, j * 128 : (j + 1) * 128].bitcast(FP8X4),
+                lhsT_scale=hscl[:, j * 128 : (j + 1) * 128],
+                rhs=w[:, cols].bitcast(FP8X4),
+                rhs_scale=ws[:, cols],
+                start=True,
+                stop=True,
+            )
+
+        def multiply(c, half):
+            for k in range(2):
+                ps = psum.tile([P, 512], F32, name="ps", tag="bank")
+                for jq in range(4):
+                    jl = k * 4 + jq
+                    o = ps[:, jq * 128 : (jq + 1) * 128]
+                    if half == 0:
+                        w0 = (jl // 2) * 2048 + c * 256 + (jl % 2) * 128
+                        one_pass(o, jl, codes0, scl0, slice(w0, w0 + 128))
+                    else:
+                        one_pass(o, 8 + jl, codes[c], scl[c], slice(jl * 128, (jl + 1) * 128))
+                banks[(c, half, k)] = ps
 
         def multiply_last(rh):
             ps = psum.tile([P, 512], F32, name="ps", tag="bank")
             for jl in range(8):
-                j = 8 + jl
-                cols = slice(rh * 512 + jl * 64, rh * 512 + (jl + 1) * 64)
-                nc.tensor.matmul_mx(
-                    out=ps[:, jl * 64 : (jl + 1) * 64],
-                    lhsT=hcodes[:, j * 128 : (j + 1) * 128].bitcast(FP8X4),
-                    lhsT_scale=hscl[:, j * 128 : (j + 1) * 128],
-                    rhs=codes[LAST][:, cols].bitcast(FP8X4),
-                    rhs_scale=scl[LAST][:, cols],
-                    start=True,
-                    stop=True,
+                w0 = rh * 512 + jl * 64
+                one_pass(ps[:, jl * 64 : (jl + 1) * 64], 8 + jl, codes[LASTC], scl[LASTC], slice(w0, w0 + 64))
+            banks[(LASTC, 1, rh)] = ps
+
+        def add_bias(c, half):
+            if half == 0:
+                osb[c] = side_tile([P, 2048], F32, "osb")
+            for k in range(2):
+                q0 = half * 64 + k * 32
+                nc.vector.tensor_tensor(
+                    out=osb[c][:].rearrange("b (r q) -> b r q", q=128)[:, :, q0 : q0 + 32],
+                    in0=banks[(c, half, k)][:].rearrange("b (q r) -> b r q", r=RC),
+                    in1=bias_c[c].rearrange("b (r q) -> b r q", q=128)[:, :, q0 : q0 + 32],
+                    op=ALU.add,
                 )
-            banks[(LAST, rh)] = ps
 
         def add_rows_last(r0, r1):
-            c = NCHUNK - 1
             rh = r0 // IR
             nc.vector.tensor_tensor(
-                out=osb[c][:].rearrange("b (r q) -> b r q", q=128)[:, r0:r1, 64:128],
-                in0=banks[(LAST, rh)][:].rearrange("b (q i) -> b i q", i=IR)[:, r0 - rh * IR : r1 - rh * IR, :],
-                in1=bias_c[c][:].rearrange("b (r q) -> b r q", q=128)[:, r0:r1, 64:128],
-                op=ALU.add,
-            )
-
-        def quantize(u, ks=(0, 1)):
-            if ks[0] == 0:
-                codes[u] = work.tile([P, 1024], U32, name="codes", tag="codes", bufs=2, align_bytes=64)
-                scl[u] = work.tile([P, 1024], U8, name="scl", tag="scl", bufs=2, align_bytes=64)
-            cols = slice(ks[0] * 512, (ks[-1] + 1) * 512)
-            nc.vector.quantize_mx(
-                out=codes[u][:, cols].bitcast(FP8X4),
-                scales=scl[u][:, cols],
-                in_=grouped[u][:, 4 * cols.start : 4 * cols.stop],
-            )
-
-        def multiply(u, ks=(0, 1)):
-            half = u % 2
-            for k in ks:
-                ps = psum.tile([P, 512], F32, name="ps", tag="bank")
-                for jq in range(4):
-                    jl = k * 4 + jq
-                    j = half * 8 + jl
-                    nc.tensor.matmul_mx(
-                        out=ps[:, jq * 128 : (jq + 1) * 128],
-                        lhsT=hcodes[:, j * 128 : (j + 1) * 128].bitcast(FP8X4),
-                        lhsT_scale=hscl[:, j * 128 : (j + 1) * 128],
-                        rhs=codes[u][:, jl * 128 : (jl + 1) * 128].bitcast(FP8X4),
-                        rhs_scale=scl[u][:, jl * 128 : (jl + 1) * 128],
-                        start=True,
-                        stop=True,
-                    )
-                banks[(u, k)] = ps
-
-        def add_rows(u, k, r0, r1):
-            c, half = divmod(u, 2)
-            q0 = half * 64 + k * 32
-            nc.vector.tensor_tensor(
-                out=osb[c][:].rearrange("b (r q) -> b r q", q=128)[:, r0:r1, q0 : q0 + 32],
-                in0=banks[(u, k)][:].rearrange("b (q r) -> b r q", r=RC)[:, r0:r1, :],
-                in1=bias_c[c][:].rearrange("b (r q) -> b r q", q=128)[:, r0:r1, q0 : q0 + 32],
+                out=osb[LASTC][:].rearrange("b (r q) -> b r q", q=128)[:, r0:r1, 64:128],
+                in0=banks[(LASTC, 1, rh)][:].rearrange("b (q i) -> b i q", i=IR)[:, r0 - rh * IR : r1 - rh * IR, :],
+                in1=bias_c[LASTC].rearrange("b (r q) -> b r q", q=128)[:, r0:r1, 64:128],
                 op=ALU.add,
             )
 
@@ -295,40 +312,106 @@ def tile_switchnet_fstar_pa_kernel(tc, x, k1_bytes, k1_scale, b1, out):
                     out=dst[:, rh, (r0 - rh * IR) * 128 : (r1 - rh * IR) * 128], in_=osb[c][:, r0 * 128 : r1 * 128]
                 )
 
-        def add_bias(u):
-            c, half = divmod(u, 2)
-            if half == 0:
-                osb[c] = side_tile([P, 2048], F32, "osb")
-            for k in range(2):
-                add_rows(u, k, 0, RC)
-            if half == 1:
-                store_rows(c, 0, RC)
-                if c + 3 < NCHUNK:
-                    load_bias(c + 3)
+        hw = {}
+        hg = {}
+        rows = {}
 
-        hw0 = gather(0)
-        hw1 = gather(1)
-        interleave(0)
-        hg0 = turn(hw0)
-        interleave(1)
-        hg1 = turn(hw1)
+        def late_row(c):
+            add_bias(c, 1)
+            store_rows(c, 0, RC)
+
+        load_bytes("E0")
+        load_bytes("E1")
+        load_bytes("L0")
+        widen("E0")
+        permute_bias()
+        load_bytes("E2")
+        load_x()
+        early_interleave(0, 0)
+        early_interleave(0, 1)
+        widen("E1")
+        load_bytes("L1")
+        load_bias(0)
+        widen("L0")
+        early_quantize(0, 0)
+        load_bytes("E3")
+        early_quantize(0, 1)
+        early_interleave(1, 0)
+        early_interleave(1, 1)
+        widen("E2")
+        load_bytes("L2")
+        early_quantize(1, 0)
+        widen("L1")
+        load_bytes("L3")
+        early_quantize(1, 1)
+        early_interleave(2, 0)
+        early_interleave(2, 1)
+        widen("E3")
+        load_bias(1)
+        hw[0] = gather(0)
+        hw[1] = gather(1)
+        early_quantize(2, 0)
+        widen("L2")
+        load_bias(2)
+        early_quantize(2, 1)
+        early_interleave(3, 0)
+        hg[0] = turn(hw[0])
+        hg[1] = turn(hw[1])
+        widen("L3")
+        load_bias(3)
+        quantize_h(0, hg[0])
+        quantize_h(1, hg[1])
+        early_quantize(3, 0)
+        late_interleave(0)
+        late_interleave(1)
+        multiply(0, 0)
+        add_bias(0, 0)
+        multiply(1, 0)
         quantize(0)
-        quantize_h(0, hg0)
-        multiply(0)
-        for s in range(LAST - 1):
-            if s + 2 < LAST:
-                interleave(s + 2)
-            else:
-                interleave_last()
-            if s == 0:
-                quantize_h(1, hg1)
-            quantize(s + 1)
-            multiply(s + 1)
-            add_bias(s)
+        multiply(0, 1)
+        add_bias(1, 0)
+        late_row(0)
+        late_interleave(2)
+        early_interleave(3, 1)
+        multiply(2, 0)
+        quantize(1)
+        multiply(1, 1)
+        add_bias(2, 0)
+        late_row(1)
+        late_interleave(3)
+        multiply(3, 0)
+        quantize(2)
+        multiply(2, 1)
+        add_bias(3, 0)
+        late_row(2)
+        late_interleave(4)
+        early_quantize(3, 1)
+        multiply(4, 0)
+        quantize(3)
+        multiply(3, 1)
+        add_bias(4, 0)
+        late_row(3)
+        late_interleave(5)
+        multiply(5, 0)
+        quantize(4)
+        multiply(4, 1)
+        add_bias(5, 0)
+        late_row(4)
+        late_interleave(6)
+        multiply(6, 0)
+        quantize(5)
+        multiply(5, 1)
+        add_bias(6, 0)
+        late_row(5)
+        late_interleave(7)
+        multiply(7, 0)
+        quantize(6)
+        multiply(6, 1)
+        add_bias(7, 0)
+        late_row(6)
         for rh in range(NRH):
-            quantize(LAST, (rh,))
+            quantize(LASTC, (rh,))
             multiply_last(rh)
-        add_bias(LAST - 1)
         for r0, r1 in LAST_ROWS:
             add_rows_last(r0, r1)
-            store_rows(NCHUNK - 1, r0, r1)
+            store_rows(LASTC, r0, r1)

@@ -22,12 +22,10 @@ NCHUNK = 128 // RC
 NJN = 128 // IR
 LASTC = NCHUNK - 1
 LAST_ROWS = [(0, 8), (8, 12), (12, 14), (14, 16)]
-S_WIDEN = {("E0", 0, 2), ("E0", 1, 1), ("E0", 1, 3), ("L1", 0, 3), ("L2", 0, 3)}
+S_WIDEN = {("E0", 0, 2): 1024, ("E0", 1, 1): 1024, ("E0", 1, 3): 1024, ("L1", 0, 3): 2048, ("L2", 0, 3): 2048}
 SPLIT = {"E0"}
 T_BLOCKS = {(0, 7), (1, 7), (2, 7), (3, 7), (1, 6), (3, 6)}
 V_BLOCKS = {(9, 9)}
-G_RUNS = [0, 0, 48, 48, 48, 48, 48, 48]
-V_RUNS = [0, 24, 0, 0, 0, 0, 0, 0]
 
 
 def tile_switchnet_fstar_pa_kernel(tc, x, k1_bytes, k1_scale, b1, out):
@@ -111,25 +109,28 @@ def tile_switchnet_fstar_pa_kernel(tc, x, k1_bytes, k1_scale, b1, out):
                     nc.sync.dma_start(out=t[:, :, jj, :], in_=src)
             kb[name] = t
 
-        def widen(name):
+        def widen(name, ts=(0, 1, 2, 3)):
             n = int(name[1:])
             if name[0] == "L":
                 dst = planes[:, :, n * 2048 : (n + 1) * 2048]
             else:
-                early[n] = pair_tile([P, 4, 2048], "early")
+                if ts[0] == 0:
+                    early[n] = pair_tile([P, 4, 2048], "early")
                 dst = early[n][:]
             parts = 2 if name in SPLIT else 1
             width = 2048 // parts
             for part in range(parts):
-                for t in range(4):
-                    cols = slice(part * width, (part + 1) * width)
-                    src = kb[name][:, t].rearrange("p jj l -> p (jj l)")[:, cols].bitcast(FP8)
-                    o = dst[:, t, cols]
-                    if (name, part, t) in S_WIDEN:
-                        nc.scalar.activation(out=o, in_=src, func=ACT.Copy, scale=sc[:, t : t + 1])
-                    else:
+                for t in ts:
+                    lo, hi = part * width, (part + 1) * width
+                    mid = hi - S_WIDEN.get((name, part, t), 0)
+                    src = kb[name][:, t].rearrange("p jj l -> p (jj l)").bitcast(FP8)
+                    if mid > lo:
                         nc.vector.tensor_scalar(
-                            out=o, in0=src, scalar1=sc[:, t : t + 1], scalar2=None, op0=ALU.mult
+                            out=dst[:, t, lo:mid], in0=src[:, lo:mid], scalar1=sc[:, t : t + 1], scalar2=None, op0=ALU.mult
+                        )
+                    if hi > mid:
+                        nc.scalar.activation(
+                            out=dst[:, t, mid:hi], in_=src[:, mid:hi], func=ACT.Copy, scale=sc[:, t : t + 1]
                         )
 
         eg = {}
@@ -162,23 +163,31 @@ def tile_switchnet_fstar_pa_kernel(tc, x, k1_bytes, k1_scale, b1, out):
             cols = slice(n * 2048 + g * 1024, n * 2048 + (g + 1) * 1024)
             nc.vector.quantize_mx(out=codes0[:, cols].bitcast(FP8X4), scales=scl0[:, cols], in_=eg[(n, g)][:])
 
-        xh = []
+        xh = {}
+        hw = {}
 
-        def load_x():
-            for hh in range(2):
-                xt = side_tile([P, 4096], BF16, "xh")
+        def load_x(hh):
+            xt = side_tile([P, 4096], BF16, "xh")
+            nc.sync.dma_start(out=xt[:], in_=x[:, hh * 2048 : (hh + 1) * 2048, :].rearrange("b n c -> b (n c)"))
+            xh[hh] = xt
+
+        def load_windows(hh, blocks):
+            if 0 in blocks:
+                hw[hh] = side_tile([P, 4096], BF16, "hw")
+            src = x[:, hh * 2048 : (hh + 1) * 2048, :].rearrange(
+                "b (g rr bc w) c -> (g bc) b rr (w c)", g=2, rr=16, bc=4, w=16
+            )
+            for blk in blocks:
                 nc.sync.dma_start(
-                    out=xt[:], in_=x[:, hh * 2048 : (hh + 1) * 2048, :].rearrange("b n c -> b (n c)")
+                    out=hw[hh][:, blk * 512 : (blk + 1) * 512].rearrange("b (rr k) -> b rr k", rr=16), in_=src[blk]
                 )
-                xh.append(xt)
 
         def gather(hh):
-            hw = side_tile([P, 2048], F32, "hw")
+            hw[hh] = side_tile([P, 4096], BF16, "hw")
             src = xh[hh][:].bitcast(F32).rearrange("b (g rr bc w) -> b g bc rr w", g=2, rr=16, bc=4, w=16)
-            dst = hw[:].rearrange("b (g bc rr w) -> b g bc rr w", g=2, bc=4, rr=16, w=16)
+            dst = hw[hh][:].bitcast(F32).rearrange("b (g bc rr w) -> b g bc rr w", g=2, bc=4, rr=16, w=16)
             for g in range(2):
                 nc.vector.tensor_copy(out=dst[:, g], in_=src[:, g])
-            return hw
 
         def turn(hw):
             hg = side_tile([P, 4096], BF16, "hg")
@@ -188,7 +197,7 @@ def tile_switchnet_fstar_pa_kernel(tc, x, k1_bytes, k1_scale, b1, out):
                 for s in range(4):
                     jl = pair * 2 + s // 2
                     nc.tensor.transpose(
-                        out=pt[:, s, :], in_=hw[:, jl * 256 + s % 2 : (jl + 1) * 256 : 2], identity=ident[:]
+                        out=pt[:, s, :], in_=hw[:].bitcast(F32)[:, jl * 256 + s % 2 : (jl + 1) * 256 : 2], identity=ident[:]
                     )
                 nc.scalar.copy(
                     out=hgw[:, 2 * pair : 2 * pair + 2],
@@ -206,38 +215,34 @@ def tile_switchnet_fstar_pa_kernel(tc, x, k1_bytes, k1_scale, b1, out):
         banks = {}
         osb = {}
 
-        def copy_runs(dst, src, g, v):
-            if g > 0:
-                nc.gpsimd.tensor_scalar(
-                    out=dst[:, :g], in0=src[:, :g], scalar1=1.0, scalar2=0.0, op0=ALU.mult, op1=ALU.add
-                )
-            n = dst.shape[1]
-            nc.scalar.copy(out=dst[:, g : n - v], in_=src[:, g : n - v])
-            if v > 0:
-                nc.vector.tensor_copy(out=dst[:, n - v :], in_=src[:, n - v :])
-
         late_buf = []
 
-        def late_interleave(c):
+        def late_tile(c):
             if not late_buf:
                 late_buf.append(pair_tile([P, 8192], "late_buf"))
-            t = late_buf[0][:, c % 2 * 4096 : (c % 2 + 1) * 4096]
+            lg[c] = late_buf[0][:, c % 2 * 4096 : (c % 2 + 1) * 4096]
+
+        def late_copy(engine, c, lo, hi):
+            views = []
             if c < LASTC:
-                copy_runs(
-                    t.rearrange("p (n i t) -> p n t i", i=IR, t=4),
-                    planes[:].rearrange("p t (n c i) -> p c n t i", c=NCHUNK, i=IR)[:, c],
-                    G_RUNS[c],
-                    V_RUNS[c],
-                )
+                views.append((
+                    lg[c].rearrange("p (n i t) -> p n t i", i=IR, t=4)[:, lo:hi],
+                    planes[:].rearrange("p t (n c i) -> p c n t i", c=NCHUNK, i=IR)[:, c, lo:hi],
+                ))
             else:
                 for rh in range(NRH):
-                    copy_runs(
-                        t.rearrange("p (rh n i t) -> p rh n t i", rh=NRH, i=IR, t=4)[:, rh],
-                        planes[:].rearrange("p t (n rh c i) -> p c rh n t i", rh=NRH, c=NCHUNK, i=IR)[:, c, rh],
-                        G_RUNS[c] // NRH,
-                        V_RUNS[c] // NRH,
-                    )
-            lg[c] = t
+                    runs = slice(lo // NRH, hi // NRH)
+                    views.append((
+                        lg[c].rearrange("p (rh n i t) -> p rh n t i", rh=NRH, i=IR, t=4)[:, rh, runs],
+                        planes[:].rearrange("p t (n rh c i) -> p c rh n t i", rh=NRH, c=NCHUNK, i=IR)[:, c, rh, runs],
+                    ))
+            for dst, src in views:
+                if engine == "gpsimd":
+                    nc.gpsimd.tensor_scalar(out=dst, in0=src, scalar1=1.0, scalar2=0.0, op0=ALU.mult, op1=ALU.add)
+                elif engine == "scalar":
+                    nc.scalar.copy(out=dst, in_=src)
+                else:
+                    nc.vector.tensor_copy(out=dst, in_=src)
 
         def quantize(c, ks=(0, 1)):
             if ks[0] == 0:
@@ -293,6 +298,20 @@ def tile_switchnet_fstar_pa_kernel(tc, x, k1_bytes, k1_scale, b1, out):
                     op=ALU.add,
                 )
 
+        def add_bias_side(c, sides=(0, 1)):
+            osb[c] = side_tile([P, 2048], F32, "osb")
+            for k in range(2):
+                q0 = k * 32
+                o = osb[c][:].rearrange("b (r q) -> b r q", q=128)[:, :, q0 : q0 + 32]
+                b = bias_c[c].rearrange("b (r q) -> b r q", q=128)[:, :, q0 : q0 + 32]
+                ps = banks[(c, 0, k)][:].rearrange("b (q r) -> b r q", r=RC)
+                if k in sides:
+                    raw = work.tile([P, 512], F32, name="raw", tag="eg", bufs=3, align_bytes=64)
+                    nc.scalar.copy(out=raw[:].rearrange("b (r q) -> b r q", q=32), in_=ps)
+                    nc.gpsimd.tensor_tensor(out=o, in0=raw[:].rearrange("b (r q) -> b r q", q=32), in1=b, op=ALU.add)
+                else:
+                    nc.vector.tensor_tensor(out=o, in0=ps, in1=b, op=ALU.add)
+
         def add_rows_last(r0, r1):
             rh = r0 // IR
             nc.vector.tensor_tensor(
@@ -312,9 +331,7 @@ def tile_switchnet_fstar_pa_kernel(tc, x, k1_bytes, k1_scale, b1, out):
                     out=dst[:, rh, (r0 - rh * IR) * 128 : (r1 - rh * IR) * 128], in_=osb[c][:, r0 * 128 : r1 * 128]
                 )
 
-        hw = {}
         hg = {}
-        rows = {}
 
         def late_row(c):
             add_bias(c, 1)
@@ -326,7 +343,8 @@ def tile_switchnet_fstar_pa_kernel(tc, x, k1_bytes, k1_scale, b1, out):
         widen("E0")
         permute_bias()
         load_bytes("E2")
-        load_x()
+        load_x(0)
+        load_x(1)
         early_interleave(0, 0)
         early_interleave(0, 1)
         widen("E1")
@@ -348,8 +366,8 @@ def tile_switchnet_fstar_pa_kernel(tc, x, k1_bytes, k1_scale, b1, out):
         early_interleave(2, 1)
         widen("E3")
         load_bias(1)
-        hw[0] = gather(0)
-        hw[1] = gather(1)
+        gather(0)
+        gather(1)
         early_quantize(2, 0)
         widen("L2")
         load_bias(2)
@@ -362,8 +380,11 @@ def tile_switchnet_fstar_pa_kernel(tc, x, k1_bytes, k1_scale, b1, out):
         quantize_h(0, hg[0])
         quantize_h(1, hg[1])
         early_quantize(3, 0)
-        late_interleave(0)
-        late_interleave(1)
+        late_tile(0)
+        late_copy("scalar", 0, 0, 128)
+        late_tile(1)
+        late_copy("scalar", 1, 0, 104)
+        late_copy("vector", 1, 104, 128)
         multiply(0, 0)
         add_bias(0, 0)
         multiply(1, 0)
@@ -371,47 +392,60 @@ def tile_switchnet_fstar_pa_kernel(tc, x, k1_bytes, k1_scale, b1, out):
         multiply(0, 1)
         add_bias(1, 0)
         late_row(0)
-        late_interleave(2)
+        late_tile(2)
+        late_copy("gpsimd", 2, 72, 128)
+        late_copy("scalar", 2, 0, 72)
         early_interleave(3, 1)
         multiply(2, 0)
         quantize(1)
         multiply(1, 1)
         add_bias(2, 0)
         late_row(1)
-        late_interleave(3)
+        late_tile(3)
+        late_copy("gpsimd", 3, 72, 128)
+        late_copy("scalar", 3, 0, 72)
         multiply(3, 0)
         quantize(2)
         multiply(2, 1)
         add_bias(3, 0)
         late_row(2)
-        late_interleave(4)
+        late_tile(4)
+        late_copy("gpsimd", 4, 72, 128)
+        late_copy("scalar", 4, 0, 72)
         early_quantize(3, 1)
         multiply(4, 0)
         quantize(3)
         multiply(3, 1)
         add_bias(4, 0)
         late_row(3)
-        late_interleave(5)
+        late_tile(5)
+        late_copy("gpsimd", 5, 72, 128)
+        late_copy("scalar", 5, 0, 72)
         multiply(5, 0)
         quantize(4)
         multiply(4, 1)
         add_bias(5, 0)
         late_row(4)
-        late_interleave(6)
+        late_tile(6)
+        late_copy("gpsimd", 6, 72, 128)
+        late_copy("scalar", 6, 0, 72)
         multiply(6, 0)
         quantize(5)
         multiply(5, 1)
         add_bias(6, 0)
         late_row(5)
-        late_interleave(7)
+        late_tile(7)
+        late_copy("gpsimd", 7, 72, 128)
+        late_copy("scalar", 7, 0, 72)
         multiply(7, 0)
         quantize(6)
         multiply(6, 1)
-        add_bias(7, 0)
+        add_bias_side(7, (1,))
         late_row(6)
-        for rh in range(NRH):
-            quantize(LASTC, (rh,))
-            multiply_last(rh)
+        quantize(LASTC, (0,))
+        multiply_last(0)
+        quantize(LASTC, (1,))
+        multiply_last(1)
         for r0, r1 in LAST_ROWS:
             add_rows_last(r0, r1)
             store_rows(LASTC, r0, r1)

@@ -22,7 +22,7 @@ NCHUNK = 128 // RC
 NJN = 128 // IR
 LASTC = NCHUNK - 1
 LAST_ROWS = [(0, 8), (8, 12), (12, 14), (14, 16)]
-S_WIDEN = {("E0", 0, 2): 1024, ("E0", 1, 1): 1024, ("E0", 1, 3): 1024, ("L1", 0, 3): 2048, ("L2", 0, 3): 2048}
+S_WIDEN = {("E0", 0, 2): 1024, ("E0", 1, 1): 1024, ("E0", 1, 3): 1024, ("L1", 0, 3): 2048, ("L3", 0, 3): 1024}
 SPLIT = {"E0"}
 T_BLOCKS = {(0, 7), (1, 7), (2, 7), (3, 7), (1, 6), (3, 6)}
 V_BLOCKS = {(9, 9)}
@@ -175,11 +175,11 @@ def tile_switchnet_fstar_pa_kernel(tc, x, k1_bytes, k1_scale, b1, out):
             if 0 in blocks:
                 hw[hh] = side_tile([P, 4096], BF16, "hw")
             src = x[:, hh * 2048 : (hh + 1) * 2048, :].rearrange(
-                "b (g rr bc w) c -> (g bc) b rr (w c)", g=2, rr=16, bc=4, w=16
+                "b (g rr bc w) c -> g bc b rr (w c)", g=2, rr=16, bc=4, w=16
             )
             for blk in blocks:
                 nc.sync.dma_start(
-                    out=hw[hh][:, blk * 512 : (blk + 1) * 512].rearrange("b (rr k) -> b rr k", rr=16), in_=src[blk]
+                    out=hw[hh][:, blk * 512 : (blk + 1) * 512].rearrange("b (rr k) -> b rr k", rr=16), in_=src[blk // 4][blk % 4]
                 )
 
         def gather(hh):
@@ -343,42 +343,44 @@ def tile_switchnet_fstar_pa_kernel(tc, x, k1_bytes, k1_scale, b1, out):
         widen("E0")
         permute_bias()
         load_bytes("E2")
-        load_x(0)
-        load_x(1)
         early_interleave(0, 0)
         early_interleave(0, 1)
         widen("E1")
         load_bytes("L1")
-        load_bias(0)
+        load_windows(0, (0,))
         widen("L0")
         early_quantize(0, 0)
         load_bytes("E3")
+        load_windows(0, (1, 2))
         early_quantize(0, 1)
         early_interleave(1, 0)
         early_interleave(1, 1)
         widen("E2")
         load_bytes("L2")
+        load_x(1)
+        load_windows(0, (3,))
         early_quantize(1, 0)
         widen("L1")
         load_bytes("L3")
+        load_windows(0, (4, 5, 6, 7))
         early_quantize(1, 1)
         early_interleave(2, 0)
         early_interleave(2, 1)
         widen("E3")
+        load_bias(0)
         load_bias(1)
-        gather(0)
-        gather(1)
         early_quantize(2, 0)
+        gather(1)
         widen("L2")
         load_bias(2)
         early_quantize(2, 1)
         early_interleave(3, 0)
-        hg[0] = turn(hw[0])
-        hg[1] = turn(hw[1])
         widen("L3")
+        hg[1] = turn(hw[1])
+        hg[0] = turn(hw[0])
         load_bias(3)
-        quantize_h(0, hg[0])
         quantize_h(1, hg[1])
+        quantize_h(0, hg[0])
         early_quantize(3, 0)
         late_tile(0)
         late_copy("scalar", 0, 0, 128)
@@ -393,8 +395,8 @@ def tile_switchnet_fstar_pa_kernel(tc, x, k1_bytes, k1_scale, b1, out):
         add_bias(1, 0)
         late_row(0)
         late_tile(2)
-        late_copy("gpsimd", 2, 72, 128)
-        late_copy("scalar", 2, 0, 72)
+        late_copy("gpsimd", 2, 80, 128)
+        late_copy("scalar", 2, 0, 80)
         early_interleave(3, 1)
         multiply(2, 0)
         quantize(1)
@@ -402,16 +404,16 @@ def tile_switchnet_fstar_pa_kernel(tc, x, k1_bytes, k1_scale, b1, out):
         add_bias(2, 0)
         late_row(1)
         late_tile(3)
-        late_copy("gpsimd", 3, 72, 128)
-        late_copy("scalar", 3, 0, 72)
+        late_copy("gpsimd", 3, 80, 128)
+        late_copy("scalar", 3, 0, 80)
         multiply(3, 0)
         quantize(2)
         multiply(2, 1)
         add_bias(3, 0)
         late_row(2)
         late_tile(4)
-        late_copy("gpsimd", 4, 72, 128)
-        late_copy("scalar", 4, 0, 72)
+        late_copy("gpsimd", 4, 80, 128)
+        late_copy("scalar", 4, 0, 80)
         early_quantize(3, 1)
         multiply(4, 0)
         quantize(3)
@@ -419,24 +421,24 @@ def tile_switchnet_fstar_pa_kernel(tc, x, k1_bytes, k1_scale, b1, out):
         add_bias(4, 0)
         late_row(3)
         late_tile(5)
-        late_copy("gpsimd", 5, 72, 128)
-        late_copy("scalar", 5, 0, 72)
+        late_copy("gpsimd", 5, 80, 128)
+        late_copy("scalar", 5, 0, 80)
         multiply(5, 0)
         quantize(4)
         multiply(4, 1)
         add_bias(5, 0)
         late_row(4)
         late_tile(6)
-        late_copy("gpsimd", 6, 72, 128)
-        late_copy("scalar", 6, 0, 72)
+        late_copy("gpsimd", 6, 80, 128)
+        late_copy("scalar", 6, 0, 80)
         multiply(6, 0)
         quantize(5)
         multiply(5, 1)
         add_bias(6, 0)
         late_row(5)
         late_tile(7)
-        late_copy("gpsimd", 7, 72, 128)
-        late_copy("scalar", 7, 0, 72)
+        late_copy("gpsimd", 7, 80, 128)
+        late_copy("scalar", 7, 0, 80)
         multiply(7, 0)
         quantize(6)
         multiply(6, 1)

@@ -21,11 +21,11 @@ NRH = RC // IR
 NCHUNK = 128 // RC
 NJN = 128 // IR
 LASTC = NCHUNK - 1
-LAST_ROWS = [(0, 8), (8, 12), (12, 14), (14, 16)]
-S_WIDEN = {("E0", 0, 2): 1024, ("E0", 1, 1): 1024, ("E0", 1, 3): 1024, ("L1", 0, 3): 2048, ("L3", 0, 3): 1024}
+ROW_CHUNKS = (99,)
+ROW_EARLY = ()
+S_WIDEN = {("E0", 0, 1): 1024, ("E0", 1, 1): 1024, ("E0", 1, 3): 1024, ("L1", 0, 3): 2048, ("L3", 0, 3): 1024}
 SPLIT = {"E0"}
 T_BLOCKS = {(0, 7), (1, 7), (2, 7), (3, 7), (1, 6), (3, 6)}
-V_BLOCKS = {(9, 9)}
 
 
 def tile_switchnet_fstar_pa_kernel(tc, x, k1_bytes, k1_scale, b1, out):
@@ -137,42 +137,51 @@ def tile_switchnet_fstar_pa_kernel(tc, x, k1_bytes, k1_scale, b1, out):
 
         def early_interleave(n, g):
             e = work.tile([P, 4096], BF16, name="eg", tag="eg", bufs=3, align_bytes=64)
-            view = early[n][:].rearrange("p t (n c i) -> p c n t i", c=NCHUNK, i=IR)
-            tview = early[n][:].rearrange("p t (n c i) -> p c n i t", c=NCHUNK, i=IR)
             for cl in range(4):
                 c = 4 * g + cl
+                parts = []
+                if c in ROW_EARLY:
+                    for rh in range(NRH):
+                        parts.append(early[n][:].rearrange("p t (n rh c i) -> p c rh n t i", rh=NRH, c=NCHUNK, i=IR)[:, c, rh])
+                else:
+                    parts.append(early[n][:].rearrange("p t (n c i) -> p c n t i", c=NCHUNK, i=IR)[:, c])
                 o = e[:, cl * 1024 : (cl + 1) * 1024]
                 if (n, c) in T_BLOCKS:
                     pp = psum.tile([P, 1024], BF16, name="pp", tag="bank")
-                    for jj in range(2):
+                    halves = parts if len(parts) == 2 else [parts[0][:, :NJN], parts[0][:, NJN:]]
+                    for q in range(2):
                         nc.tensor.matmul(
-                            out=pp[:, jj * 512 : (jj + 1) * 512].rearrange("p (n i t) -> p n i t", i=IR, t=4),
+                            out=pp[:, q * 512 : (q + 1) * 512].rearrange("p (n i t) -> p n i t", i=IR, t=4),
                             lhsT=ident_bf[:],
-                            rhs=tview[:, c, jj * NJN : (jj + 1) * NJN],
+                            rhs=halves[q].rearrange("p n t i -> p n i t"),
                             start=True,
                             stop=True,
                         )
                     nc.scalar.copy(out=o, in_=pp[:])
-                elif (n, c) in V_BLOCKS:
-                    nc.vector.tensor_copy(out=o.rearrange("p (n i t) -> p n t i", i=IR, t=4), in_=view[:, c])
                 else:
-                    nc.scalar.copy(out=o.rearrange("p (n i t) -> p n t i", i=IR, t=4), in_=view[:, c])
+                    width = 1024 // len(parts)
+                    for q, src in enumerate(parts):
+                        nc.scalar.copy(
+                            out=o[:, q * width : (q + 1) * width].rearrange("p (n i t) -> p n t i", i=IR, t=4), in_=src
+                        )
             eg[(n, g)] = e
 
         def early_quantize(n, g):
             cols = slice(n * 2048 + g * 1024, n * 2048 + (g + 1) * 1024)
             nc.vector.quantize_mx(out=codes0[:, cols].bitcast(FP8X4), scales=scl0[:, cols], in_=eg[(n, g)][:])
 
-        xh = {}
+        xg = {}
         hw = {}
 
-        def load_x(hh):
-            xt = side_tile([P, 4096], BF16, "xh")
-            nc.sync.dma_start(out=xt[:], in_=x[:, hh * 2048 : (hh + 1) * 2048, :].rearrange("b n c -> b (n c)"))
-            xh[hh] = xt
+        def load_x(hh, gs):
+            r0 = (2 * hh + gs[0]) * 1024
+            xt = side_tile([P, 2048 * len(gs)], BF16, "xg")
+            nc.sync.dma_start(out=xt[:], in_=x[:, r0 : r0 + 1024 * len(gs), :].rearrange("b n c -> b (n c)"))
+            for q, g in enumerate(gs):
+                xg[(hh, g)] = xt[:, q * 2048 : (q + 1) * 2048]
 
         def load_windows(hh, blocks):
-            if 0 in blocks:
+            if hh not in hw:
                 hw[hh] = side_tile([P, 4096], BF16, "hw")
             src = x[:, hh * 2048 : (hh + 1) * 2048, :].rearrange(
                 "b (g rr bc w) c -> g bc b rr (w c)", g=2, rr=16, bc=4, w=16
@@ -182,12 +191,13 @@ def tile_switchnet_fstar_pa_kernel(tc, x, k1_bytes, k1_scale, b1, out):
                     out=hw[hh][:, blk * 512 : (blk + 1) * 512].rearrange("b (rr k) -> b rr k", rr=16), in_=src[blk // 4][blk % 4]
                 )
 
-        def gather(hh):
-            hw[hh] = side_tile([P, 4096], BF16, "hw")
-            src = xh[hh][:].bitcast(F32).rearrange("b (g rr bc w) -> b g bc rr w", g=2, rr=16, bc=4, w=16)
+        def gather(hh, g):
+            if hh not in hw:
+                hw[hh] = side_tile([P, 4096], BF16, "hw")
+            xt = xg[(hh, g)]
+            src = xt.bitcast(F32).rearrange("b (rr bc w) -> b bc rr w", rr=16, bc=4, w=16)
             dst = hw[hh][:].bitcast(F32).rearrange("b (g bc rr w) -> b g bc rr w", g=2, bc=4, rr=16, w=16)
-            for g in range(2):
-                nc.vector.tensor_copy(out=dst[:, g], in_=src[:, g])
+            nc.vector.tensor_copy(out=dst[:, g], in_=src)
 
         def turn(hw):
             hg = side_tile([P, 4096], BF16, "hg")
@@ -224,7 +234,7 @@ def tile_switchnet_fstar_pa_kernel(tc, x, k1_bytes, k1_scale, b1, out):
 
         def late_copy(engine, c, lo, hi):
             views = []
-            if c < LASTC:
+            if c not in ROW_CHUNKS:
                 views.append((
                     lg[c].rearrange("p (n i t) -> p n t i", i=IR, t=4)[:, lo:hi],
                     planes[:].rearrange("p t (n c i) -> p c n t i", c=NCHUNK, i=IR)[:, c, lo:hi],
@@ -279,12 +289,48 @@ def tile_switchnet_fstar_pa_kernel(tc, x, k1_bytes, k1_scale, b1, out):
                         one_pass(o, 8 + jl, codes[c], scl[c], slice(jl * 128, (jl + 1) * 128))
                 banks[(c, half, k)] = ps
 
-        def multiply_last(rh):
+        def multiply_bank(c, half, k):
+            ps = psum.tile([P, 512], F32, name="ps", tag="bank")
+            for jq in range(4):
+                jl = k * 4 + jq
+                one_pass(ps[:, jq * 128 : (jq + 1) * 128], 8 * half + jl, codes[c], scl[c], slice(jl * 128, (jl + 1) * 128))
+            banks[(c, half, k)] = ps
+
+        def add_bank(c, half, k, r0, r1):
+            q0 = half * 64 + k * 32
+            nc.vector.tensor_tensor(
+                out=osb[c][:].rearrange("b (r q) -> b r q", q=128)[:, r0:r1, q0 : q0 + 32],
+                in0=banks[(c, half, k)][:].rearrange("b (q r) -> b r q", r=RC)[:, r0:r1, :],
+                in1=bias_c[c].rearrange("b (r q) -> b r q", q=128)[:, r0:r1, q0 : q0 + 32],
+                op=ALU.add,
+            )
+
+        def add_bank_side(c, k):
+            if c not in osb:
+                osb[c] = side_tile([P, 2048], F32, "osb")
+            q0 = k * 32
+            raw = work.tile([P, 512], F32, name="raw", tag="eg", bufs=3, align_bytes=64)
+            nc.scalar.copy(
+                out=raw[:].rearrange("b (r q) -> b r q", q=32), in_=banks[(c, 0, k)][:].rearrange("b (q r) -> b r q", r=RC)
+            )
+            nc.gpsimd.tensor_tensor(
+                out=osb[c][:].rearrange("b (r q) -> b r q", q=128)[:, :, q0 : q0 + 32],
+                in0=raw[:].rearrange("b (r q) -> b r q", q=32),
+                in1=bias_c[c].rearrange("b (r q) -> b r q", q=128)[:, :, q0 : q0 + 32],
+                op=ALU.add,
+            )
+
+        def multiply_rows(c, half, rh):
             ps = psum.tile([P, 512], F32, name="ps", tag="bank")
             for jl in range(8):
-                w0 = rh * 512 + jl * 64
-                one_pass(ps[:, jl * 64 : (jl + 1) * 64], 8 + jl, codes[LASTC], scl[LASTC], slice(w0, w0 + 64))
-            banks[(LASTC, 1, rh)] = ps
+                o = ps[:, jl * 64 : (jl + 1) * 64]
+                if half == 0:
+                    w0 = (jl // 2) * 2048 + c * 256 + rh * 128 + (jl % 2) * 64
+                    one_pass(o, jl, codes0, scl0, slice(w0, w0 + 64))
+                else:
+                    w0 = rh * 512 + jl * 64
+                    one_pass(o, 8 + jl, codes[c], scl[c], slice(w0, w0 + 64))
+            banks[(c, half, rh)] = ps
 
         def add_bias(c, half):
             if half == 0:
@@ -298,26 +344,29 @@ def tile_switchnet_fstar_pa_kernel(tc, x, k1_bytes, k1_scale, b1, out):
                     op=ALU.add,
                 )
 
-        def add_bias_side(c, sides=(0, 1)):
-            osb[c] = side_tile([P, 2048], F32, "osb")
-            for k in range(2):
-                q0 = k * 32
-                o = osb[c][:].rearrange("b (r q) -> b r q", q=128)[:, :, q0 : q0 + 32]
-                b = bias_c[c].rearrange("b (r q) -> b r q", q=128)[:, :, q0 : q0 + 32]
-                ps = banks[(c, 0, k)][:].rearrange("b (q r) -> b r q", r=RC)
-                if k in sides:
-                    raw = work.tile([P, 512], F32, name="raw", tag="eg", bufs=3, align_bytes=64)
-                    nc.scalar.copy(out=raw[:].rearrange("b (r q) -> b r q", q=32), in_=ps)
-                    nc.gpsimd.tensor_tensor(out=o, in0=raw[:].rearrange("b (r q) -> b r q", q=32), in1=b, op=ALU.add)
-                else:
-                    nc.vector.tensor_tensor(out=o, in0=ps, in1=b, op=ALU.add)
-
-        def add_rows_last(r0, r1):
+        def add_rows(c, half, r0, r1):
+            if c not in osb:
+                osb[c] = side_tile([P, 2048], F32, "osb")
             rh = r0 // IR
+            cols = slice(half * 64, half * 64 + 64)
             nc.vector.tensor_tensor(
-                out=osb[LASTC][:].rearrange("b (r q) -> b r q", q=128)[:, r0:r1, 64:128],
-                in0=banks[(LASTC, 1, rh)][:].rearrange("b (q i) -> b i q", i=IR)[:, r0 - rh * IR : r1 - rh * IR, :],
-                in1=bias_c[LASTC].rearrange("b (r q) -> b r q", q=128)[:, r0:r1, 64:128],
+                out=osb[c][:].rearrange("b (r q) -> b r q", q=128)[:, r0:r1, cols],
+                in0=banks[(c, half, rh)][:].rearrange("b (q i) -> b i q", i=IR)[:, r0 - rh * IR : r1 - rh * IR, :],
+                in1=bias_c[c].rearrange("b (r q) -> b r q", q=128)[:, r0:r1, cols],
+                op=ALU.add,
+            )
+
+        def add_rows_side(c, rh):
+            if c not in osb:
+                osb[c] = side_tile([P, 2048], F32, "osb")
+            raw = work.tile([P, 512], F32, name="raw", tag="eg", bufs=3, align_bytes=64)
+            nc.scalar.copy(
+                out=raw[:].rearrange("b (i q) -> b i q", i=IR), in_=banks[(c, 0, rh)][:].rearrange("b (q i) -> b i q", i=IR)
+            )
+            nc.gpsimd.tensor_tensor(
+                out=osb[c][:].rearrange("b (r q) -> b r q", q=128)[:, rh * IR : (rh + 1) * IR, 0:64],
+                in0=raw[:].rearrange("b (i q) -> b i q", i=IR),
+                in1=bias_c[c].rearrange("b (r q) -> b r q", q=128)[:, rh * IR : (rh + 1) * IR, 0:64],
                 op=ALU.add,
             )
 
@@ -357,7 +406,7 @@ def tile_switchnet_fstar_pa_kernel(tc, x, k1_bytes, k1_scale, b1, out):
         early_interleave(1, 1)
         widen("E2")
         load_bytes("L2")
-        load_x(1)
+        load_x(1, (0, 1))
         load_windows(0, (3,))
         early_quantize(1, 0)
         widen("L1")
@@ -370,7 +419,8 @@ def tile_switchnet_fstar_pa_kernel(tc, x, k1_bytes, k1_scale, b1, out):
         load_bias(0)
         load_bias(1)
         early_quantize(2, 0)
-        gather(1)
+        gather(1, 0)
+        gather(1, 1)
         widen("L2")
         load_bias(2)
         early_quantize(2, 1)
@@ -385,8 +435,8 @@ def tile_switchnet_fstar_pa_kernel(tc, x, k1_bytes, k1_scale, b1, out):
         late_tile(0)
         late_copy("scalar", 0, 0, 128)
         late_tile(1)
-        late_copy("scalar", 1, 0, 104)
-        late_copy("vector", 1, 104, 128)
+        late_copy("scalar", 1, 0, 96)
+        late_copy("vector", 1, 96, 128)
         multiply(0, 0)
         add_bias(0, 0)
         multiply(1, 0)
@@ -432,22 +482,26 @@ def tile_switchnet_fstar_pa_kernel(tc, x, k1_bytes, k1_scale, b1, out):
         late_copy("gpsimd", 6, 80, 128)
         late_copy("scalar", 6, 0, 80)
         multiply(6, 0)
+        multiply(7, 0)
         quantize(5)
         multiply(5, 1)
         add_bias(6, 0)
         late_row(5)
         late_tile(7)
         late_copy("gpsimd", 7, 80, 128)
-        late_copy("scalar", 7, 0, 80)
-        multiply(7, 0)
+        late_copy("scalar", 7, 0, 64)
+        late_copy("scalar", 7, 64, 80)
         quantize(6)
         multiply(6, 1)
-        add_bias_side(7, (1,))
+        add_bank_side(7, 1)
+        add_bank(7, 0, 0, 0, 16)
         late_row(6)
-        quantize(LASTC, (0,))
-        multiply_last(0)
-        quantize(LASTC, (1,))
-        multiply_last(1)
-        for r0, r1 in LAST_ROWS:
-            add_rows_last(r0, r1)
-            store_rows(LASTC, r0, r1)
+        quantize(7, (0,))
+        multiply_bank(7, 1, 0)
+        quantize(7, (1,))
+        multiply_bank(7, 1, 1)
+        add_bank(7, 1, 0, 0, 16)
+        add_bank(7, 1, 1, 0, 8)
+        store_rows(7, 0, 8)
+        add_bank(7, 1, 1, 8, 16)
+        store_rows(7, 8, 16)

@@ -247,7 +247,18 @@ def tile_switchnet_fstar_pa_kernel(tc, x, k1_bytes, k1_scale, b1, out):
                         planes[:].rearrange("p t (n rh c i) -> p c rh n t i", rh=NRH, c=NCHUNK, i=IR)[:, c, rh, runs],
                     ))
             for dst, src in views:
-                if engine == "gpsimd":
+                if engine == "tensor":
+                    pp = psum.tile([P, 1024], BF16, name="pp", tag="bank")
+                    for q in range(0, hi - lo, NJN):
+                        nc.tensor.matmul(
+                            out=pp[:, q * 32 : (q + NJN) * 32].rearrange("p (n i t) -> p n i t", i=IR, t=4),
+                            lhsT=ident_bf[:],
+                            rhs=src[:, q : q + NJN].rearrange("p n t i -> p n i t"),
+                            start=True,
+                            stop=True,
+                        )
+                    nc.scalar.copy(out=lg[c][:, lo * 32 : hi * 32], in_=pp[:, : (hi - lo) * 32])
+                elif engine == "gpsimd":
                     nc.gpsimd.tensor_scalar(out=dst, in0=src, scalar1=1.0, scalar2=0.0, op0=ALU.mult, op1=ALU.add)
                 elif engine == "scalar":
                     nc.scalar.copy(out=dst, in_=src)
@@ -309,13 +320,13 @@ def tile_switchnet_fstar_pa_kernel(tc, x, k1_bytes, k1_scale, b1, out):
             if c not in osb:
                 osb[c] = side_tile([P, 2048], F32, "osb")
             q0 = k * 32
-            raw = work.tile([P, 512], F32, name="raw", tag="eg", bufs=3, align_bytes=64)
+            raw = lg[c - 1].bitcast(F32)[:, k * 512 : (k + 1) * 512]
             nc.scalar.copy(
-                out=raw[:].rearrange("b (r q) -> b r q", q=32), in_=banks[(c, 0, k)][:].rearrange("b (q r) -> b r q", r=RC)
+                out=raw.rearrange("b (r q) -> b r q", q=32), in_=banks[(c, 0, k)][:].rearrange("b (q r) -> b r q", r=RC)
             )
             nc.gpsimd.tensor_tensor(
                 out=osb[c][:].rearrange("b (r q) -> b r q", q=128)[:, :, q0 : q0 + 32],
-                in0=raw[:].rearrange("b (r q) -> b r q", q=32),
+                in0=raw.rearrange("b (r q) -> b r q", q=32),
                 in1=bias_c[c].rearrange("b (r q) -> b r q", q=128)[:, :, q0 : q0 + 32],
                 op=ALU.add,
             )
@@ -489,17 +500,14 @@ def tile_switchnet_fstar_pa_kernel(tc, x, k1_bytes, k1_scale, b1, out):
         late_row(5)
         late_tile(7)
         late_copy("gpsimd", 7, 80, 128)
-        late_copy("scalar", 7, 0, 64)
-        late_copy("scalar", 7, 64, 80)
+        late_copy("scalar", 7, 0, 80)
         quantize(6)
         multiply(6, 1)
+        quantize(7)
+        multiply(7, 1)
         add_bank_side(7, 1)
-        add_bank(7, 0, 0, 0, 16)
         late_row(6)
-        quantize(7, (0,))
-        multiply_bank(7, 1, 0)
-        quantize(7, (1,))
-        multiply_bank(7, 1, 1)
+        add_bank(7, 0, 0, 0, 16)
         add_bank(7, 1, 0, 0, 16)
         add_bank(7, 1, 1, 0, 8)
         store_rows(7, 0, 8)

from contextlib import ExitStack

import concourse.masks as masks
import concourse.mybir as mybir

FLOPS = 2 * 128 * 16 * 512 * 1024

F32 = mybir.dt.float32
BF16 = mybir.dt.bfloat16
U32 = mybir.dt.uint32
U8 = mybir.dt.uint8
FP8 = mybir.dt.float8_e4m3fn
FP8X4 = mybir.dt.float8_e4m3fn_x4
ACT = mybir.ActivationFunctionType
ALU = mybir.AluOpType

P = 128
RC = 16
IR = 8
NRH = RC // IR
NCHUNK = 128 // RC
NJN = 128 // IR
LASTC = NCHUNK - 1
ROW_CHUNKS = (99,)
ROW_EARLY = ()
S_WIDEN = {("E0", 0, 1): 1024, ("E0", 1, 1): 1024, ("E0", 1, 3): 1024, ("L1", 0, 3): 2048, ("L3", 0, 3): 1024}
SPLIT = {"E0"}
T_BLOCKS = {(0, 7), (1, 7), (2, 7), (3, 7), (1, 6), (3, 6)}


def tile_switchnet_fstar_pa_kernel(tc, x, k1_bytes, k1_scale, b1, out):
    nc = tc.nc
    with ExitStack() as ctx:
        keep = ctx.enter_context(tc.tile_pool(name="keep", bufs=1))
        work = ctx.enter_context(tc.tile_pool(name="work", bufs=2))
        psum = ctx.enter_context(tc.psum_pool(name="psum", bufs=8))
        ctx.enter_context(tc.manual_schedule())

        planes = keep.tile([P, 4, 8192], BF16, name="planes")
        codes0 = keep.tile([P, 8192], U32, name="codes0", align_bytes=64)
        scl0 = keep.tile([P, 8192], U8, name="scl0", align_bytes=64)
        b_nat = keep.tile([P, P], BF16, name="b_nat")
        b_f32 = keep.tile([P, P], F32, name="b_f32")
        b_t = keep.tile([P, P], BF16, name="b_t")
        hcodes = keep.tile([P, 2048], U32, name="hcodes", align_bytes=64)
        hscl = keep.tile([P, 2048], U8, name="hscl", align_bytes=64)
        ident = keep.tile([P, P], F32, name="ident")
        ident_bf = keep.tile([P, P], BF16, name="ident_bf")
        sc = keep.tile([P, 4], F32, name="sc")
        warm = keep.tile([P, 2], F32, name="warm")

        nc.scalar.dma_start(out=sc[:], in_=k1_scale.rearrange("o (p t) x -> p (o t x)", t=4))
        nc.scalar.dma_start(out=b_nat[:], in_=b1.rearrange("o j (m r) -> (o j m) r", r=128))
        nc.vector.memset(warm[:], 0.0)
        nc.scalar.activation(out=warm[:, 1:2], in_=warm[:, 0:1], func=ACT.Copy)
        masks.make_identity(nc, ident[:])
        masks.make_identity(nc, ident_bf[:])

        scratch = out[127].rearrange("r q -> (r q)").bitcast(BF16)[0:16384]

        def permute_bias():
            nc.vector.tensor_copy(
                out=b_f32[:].rearrange("q (c rh i) -> q c rh i", c=NCHUNK, rh=NRH, i=IR),
                in_=b_nat[:].rearrange("q (rh c i) -> q c rh i", rh=NRH, c=NCHUNK, i=IR),
            )
            pb = psum.tile([P, 4, 128], F32, name="pb", tag="bank")
            nc.tensor.transpose(out=pb[:, 0, :], in_=b_f32[:], identity=ident[:])
            nc.scalar.copy(out=b_t[:], in_=pb[:, 0, :])
            nc.scalar.dma_start(out=scratch.rearrange("(w q) -> w q", q=128), in_=b_t[:])

        bias_c = {}

        def load_bias(b):
            if b == 0:
                bt = keep.tile([P, 4096], BF16, name="bias_0", align_bytes=64)
            else:
                bt = work.tile([P, 4096], BF16, name="bias_c", tag="bytes", bufs=3, align_bytes=64)
            nc.sync.dma_start(out=bt[:], in_=scratch.rearrange("(b x) -> b x", b=NCHUNK // 2)[b].partition_broadcast(P))
            for e in range(2):
                bias_c[2 * b + e] = bt[:, e * 2048 : (e + 1) * 2048]

        def side_tile(shape, dtype, name):
            return work.tile(shape, dtype, name=name, tag="side", bufs=3, align_bytes=64)

        def pair_tile(shape, name):
            return work.tile(shape, BF16, name=name, tag="pair", bufs=2, align_bytes=64)

        kb = {}
        early = {}

        def load_bytes(name):
            n = int(name[1:])
            j0 = 2 * n if name[0] == "E" else 8 + 2 * n
            t = work.tile([P, 4, 2, 1024], U8, name="k1b", tag="bytes", bufs=3, align_bytes=64)
            for jj in range(2):
                src = k1_bytes[j0 + jj].rearrange("(p t) l -> p t l", t=4)
                if name == "E0" and jj == 0:
                    for tt in range(4):
                        nc.sync.dma_start(out=t[:, tt, jj, :], in_=src[:, tt, :])
                elif name == "E0":
                    for tt in range(0, 4, 2):
                        nc.sync.dma_start(out=t[:, tt : tt + 2, jj, :], in_=src[:, tt : tt + 2, :])
                elif name == "E1":
                    if jj == 0:
                        both = k1_bytes[j0 : j0 + 2].rearrange("jj (p t) l -> p t jj l", t=4)
                        for tt in range(4):
                            nc.sync.dma_start(out=t[:, tt], in_=both[:, tt])
                else:
                    nc.sync.dma_start(out=t[:, :, jj, :], in_=src)
            kb[name] = t

        def widen(name, ts=(0, 1, 2, 3)):
            n = int(name[1:])
            if name[0] == "L":
                dst = planes[:, :, n * 2048 : (n + 1) * 2048]
            else:
                if ts[0] == 0:
                    early[n] = pair_tile([P, 4, 2048], "early")
                dst = early[n][:]
            parts = 2 if name in SPLIT else 1
            width = 2048 // parts
            for part in range(parts):
                for t in ts:
                    lo, hi = part * width, (part + 1) * width
                    mid = hi - S_WIDEN.get((name, part, t), 0)
                    src = kb[name][:, t].rearrange("p jj l -> p (jj l)").bitcast(FP8)
                    if mid > lo:
                        nc.vector.tensor_scalar(
                            out=dst[:, t, lo:mid], in0=src[:, lo:mid], scalar1=sc[:, t : t + 1], scalar2=None, op0=ALU.mult
                        )
                    if hi > mid:
                        nc.scalar.activation(
                            out=dst[:, t, mid:hi], in_=src[:, mid:hi], func=ACT.Copy, scale=sc[:, t : t + 1]
                        )

        eg = {}

        def early_interleave(n, g):
            e = work.tile([P, 4096], BF16, name="eg", tag="eg", bufs=3, align_bytes=64)
            for cl in range(4):
                c = 4 * g + cl
                parts = []
                if c in ROW_EARLY:
                    for rh in range(NRH):
                        parts.append(early[n][:].rearrange("p t (n rh c i) -> p c rh n t i", rh=NRH, c=NCHUNK, i=IR)[:, c, rh])
                else:
                    parts.append(early[n][:].rearrange("p t (n c i) -> p c n t i", c=NCHUNK, i=IR)[:, c])
                o = e[:, cl * 1024 : (cl + 1) * 1024]
                if (n, c) in T_BLOCKS:
                    pp = psum.tile([P, 1024], BF16, name="pp", tag="bank")
                    halves = parts if len(parts) == 2 else [parts[0][:, :NJN], parts[0][:, NJN:]]
                    for q in range(2):
                        nc.tensor.matmul(
                            out=pp[:, q * 512 : (q + 1) * 512].rearrange("p (n i t) -> p n i t", i=IR, t=4),
                            lhsT=ident_bf[:],
                            rhs=halves[q].rearrange("p n t i -> p n i t"),
                            start=True,
                            stop=True,
                        )
                    nc.scalar.copy(out=o, in_=pp[:])
                else:
                    width = 1024 // len(parts)
                    for q, src in enumerate(parts):
                        nc.scalar.copy(
                            out=o[:, q * width : (q + 1) * width].rearrange("p (n i t) -> p n t i", i=IR, t=4), in_=src
                        )
            eg[(n, g)] = e

        def early_quantize(n, g):
            cols = slice(n * 2048 + g * 1024, n * 2048 + (g + 1) * 1024)
            nc.vector.quantize_mx(out=codes0[:, cols].bitcast(FP8X4), scales=scl0[:, cols], in_=eg[(n, g)][:])

        xg = {}
        hw = {}

        def load_x(hh, gs):
            r0 = (2 * hh + gs[0]) * 1024
            xt = side_tile([P, 2048 * len(gs)], BF16, "xg")
            nc.sync.dma_start(out=xt[:], in_=x[:, r0 : r0 + 1024 * len(gs), :].rearrange("b n c -> b (n c)"))
            for q, g in enumerate(gs):
                xg[(hh, g)] = xt[:, q * 2048 : (q + 1) * 2048]

        def load_windows(hh, blocks):
            if hh not in hw:
                hw[hh] = side_tile([P, 4096], BF16, "hw")
            src = x[:, hh * 2048 : (hh + 1) * 2048, :].rearrange(
                "b (g rr bc w) c -> g bc b rr (w c)", g=2, rr=16, bc=4, w=16
            )
            for blk in blocks:
                nc.sync.dma_start(
                    out=hw[hh][:, blk * 512 : (blk + 1) * 512].rearrange("b (rr k) -> b rr k", rr=16), in_=src[blk // 4][blk % 4]
                )

        def gather(hh, g):
            if hh not in hw:
                hw[hh] = side_tile([P, 4096], BF16, "hw")
            xt = xg[(hh, g)]
            src = xt.bitcast(F32).rearrange("b (rr bc w) -> b bc rr w", rr=16, bc=4, w=16)
            dst = hw[hh][:].bitcast(F32).rearrange("b (g bc rr w) -> b g bc rr w", g=2, bc=4, rr=16, w=16)
            nc.vector.tensor_copy(out=dst[:, g], in_=src)

        def turn(hw):
            hg = side_tile([P, 4096], BF16, "hg")
            hgw = hg[:].bitcast(F32).rearrange("p (jl b u) -> p jl b u", jl=8, b=128, u=2)
            for pair in range(4):
                pt = psum.tile([P, 4, 128], F32, name="pt", tag="bank")
                for s in range(4):
                    jl = pair * 2 + s // 2
                    nc.tensor.transpose(
                        out=pt[:, s, :], in_=hw[:].bitcast(F32)[:, jl * 256 + s % 2 : (jl + 1) * 256 : 2], identity=ident[:]
                    )
                nc.scalar.copy(
                    out=hgw[:, 2 * pair : 2 * pair + 2],
                    in_=pt[:].rearrange("p (jl u) b -> p jl b u", u=2),
                )
            return hg

        def quantize_h(hh, hg):
            cols = slice(hh * 1024, (hh + 1) * 1024)
            nc.vector.quantize_mx(out=hcodes[:, cols].bitcast(FP8X4), scales=hscl[:, cols], in_=hg[:])

        lg = {}
        codes = {}
        scl = {}
        banks = {}
        osb = {}

        late_buf = []

        def late_tile(c):
            if not late_buf:
                late_buf.append(pair_tile([P, 8192], "late_buf"))
            lg[c] = late_buf[0][:, c % 2 * 4096 : (c % 2 + 1) * 4096]

        def late_copy(engine, c, lo, hi):
            views = []
            if c not in ROW_CHUNKS:
                views.append((
                    lg[c].rearrange("p (n i t) -> p n t i", i=IR, t=4)[:, lo:hi],
                    planes[:].rearrange("p t (n c i) -> p c n t i", c=NCHUNK, i=IR)[:, c, lo:hi],
                ))
            else:
                for rh in range(NRH):
                    runs = slice(lo // NRH, hi // NRH)
                    views.append((
                        lg[c].rearrange("p (rh n i t) -> p rh n t i", rh=NRH, i=IR, t=4)[:, rh, runs],
                        planes[:].rearrange("p t (n rh c i) -> p c rh n t i", rh=NRH, c=NCHUNK, i=IR)[:, c, rh, runs],
                    ))
            for dst, src in views:
                if engine == "tensor":
                    pp = psum.tile([P, 1024], BF16, name="pp", tag="bank")
                    for q in range(0, hi - lo, NJN):
                        nc.tensor.matmul(
                            out=pp[:, q * 32 : (q + NJN) * 32].rearrange("p (n i t) -> p n i t", i=IR, t=4),
                            lhsT=ident_bf[:],
                            rhs=src[:, q : q + NJN].rearrange("p n t i -> p n i t"),
                            start=True,
                            stop=True,
                        )
                    nc.scalar.copy(out=lg[c][:, lo * 32 : hi * 32], in_=pp[:, : (hi - lo) * 32])
                elif engine == "gpsimd":
                    nc.gpsimd.tensor_scalar(out=dst, in0=src, scalar1=1.0, scalar2=0.0, op0=ALU.mult, op1=ALU.add)
                elif engine == "scalar":
                    nc.scalar.copy(out=dst, in_=src)
                else:
                    nc.vector.tensor_copy(out=dst, in_=src)

        def quantize(c, ks=(0, 1)):
            if ks[0] == 0:
                codes[c] = work.tile([P, 1024], U32, name="codes", tag="codes", bufs=2, align_bytes=64)
                scl[c] = work.tile([P, 1024], U8, name="scl", tag="scl", bufs=2, align_bytes=64)
            cols = slice(ks[0] * 512, (ks[-1] + 1) * 512)
            nc.vector.quantize_mx(
                out=codes[c][:, cols].bitcast(FP8X4),
                scales=scl[c][:, cols],
                in_=lg[c][:, 4 * cols.start : 4 * cols.stop],
            )

        def one_pass(out_ap, j, w, ws, cols):
            nc.tensor.matmul_mx(
                out=out_ap,
                lhsT=hcodes[:, j * 128 : (j + 1) * 128].bitcast(FP8X4),
                lhsT_scale=hscl[:, j * 128 : (j + 1) * 128],
                rhs=w[:, cols].bitcast(FP8X4),
                rhs_scale=ws[:, cols],
                start=True,
                stop=True,
            )

        def multiply(c, half):
            for k in range(2):
                ps = psum.tile([P, 512], F32, name="ps", tag="bank")
                for jq in range(4):
                    jl = k * 4 + jq
                    o = ps[:, jq * 128 : (jq + 1) * 128]
                    if half == 0:
                        w0 = (jl // 2) * 2048 + c * 256 + (jl % 2) * 128
                        one_pass(o, jl, codes0, scl0, slice(w0, w0 + 128))
                    else:
                        one_pass(o, 8 + jl, codes[c], scl[c], slice(jl * 128, (jl + 1) * 128))
                banks[(c, half, k)] = ps

        def multiply_bank(c, half, k):
            ps = psum.tile([P, 512], F32, name="ps", tag="bank")
            for jq in range(4):
                jl = k * 4 + jq
                one_pass(ps[:, jq * 128 : (jq + 1) * 128], 8 * half + jl, codes[c], scl[c], slice(jl * 128, (jl + 1) * 128))
            banks[(c, half, k)] = ps

        def add_bank(c, half, k, r0, r1):
            q0 = half * 64 + k * 32
            nc.vector.tensor_tensor(
                out=osb[c][:].rearrange("b (r q) -> b r q", q=128)[:, r0:r1, q0 : q0 + 32],
                in0=banks[(c, half, k)][:].rearrange("b (q r) -> b r q", r=RC)[:, r0:r1, :],
                in1=bias_c[c].rearrange("b (r q) -> b r q", q=128)[:, r0:r1, q0 : q0 + 32],
                op=ALU.add,
            )

        def add_bank_side(c, k):
            if c not in osb:
                osb[c] = side_tile([P, 2048], F32, "osb")
            q0 = k * 32
            raw = lg[c - 1].bitcast(F32)[:, k * 512 : (k + 1) * 512]
            nc.scalar.copy(
                out=raw.rearrange("b (r q) -> b r q", q=32), in_=banks[(c, 0, k)][:].rearrange("b (q r) -> b r q", r=RC)
            )
            nc.gpsimd.tensor_tensor(
                out=osb[c][:].rearrange("b (r q) -> b r q", q=128)[:, :, q0 : q0 + 32],
                in0=raw.rearrange("b (r q) -> b r q", q=32),
                in1=bias_c[c].rearrange("b (r q) -> b r q", q=128)[:, :, q0 : q0 + 32],
                op=ALU.add,
            )

        def multiply_rows(c, half, rh):
            ps = psum.tile([P, 512], F32, name="ps", tag="bank")
            for jl in range(8):
                o = ps[:, jl * 64 : (jl + 1) * 64]
                if half == 0:
                    w0 = (jl // 2) * 2048 + c * 256 + rh * 128 + (jl % 2) * 64
                    one_pass(o, jl, codes0, scl0, slice(w0, w0 + 64))
                else:
                    w0 = rh * 512 + jl * 64
                    one_pass(o, 8 + jl, codes[c], scl[c], slice(w0, w0 + 64))
            banks[(c, half, rh)] = ps

        def add_bias(c, half):
            if half == 0:
                osb[c] = side_tile([P, 2048], F32, "osb")
            for k in range(2):
                q0 = half * 64 + k * 32
                nc.vector.tensor_tensor(
                    out=osb[c][:].rearrange("b (r q) -> b r q", q=128)[:, :, q0 : q0 + 32],
                    in0=banks[(c, half, k)][:].rearrange("b (q r) -> b r q", r=RC),
                    in1=bias_c[c].rearrange("b (r q) -> b r q", q=128)[:, :, q0 : q0 + 32],
                    op=ALU.add,
                )

        def add_rows(c, half, r0, r1):
            if c not in osb:
                osb[c] = side_tile([P, 2048], F32, "osb")
            rh = r0 // IR
            cols = slice(half * 64, half * 64 + 64)
            nc.vector.tensor_tensor(
                out=osb[c][:].rearrange("b (r q) -> b r q", q=128)[:, r0:r1, cols],
                in0=banks[(c, half, rh)][:].rearrange("b (q i) -> b i q", i=IR)[:, r0 - rh * IR : r1 - rh * IR, :],
                in1=bias_c[c].rearrange("b (r q) -> b r q", q=128)[:, r0:r1, cols],
                op=ALU.add,
            )

        def add_rows_side(c, rh):
            if c not in osb:
                osb[c] = side_tile([P, 2048], F32, "osb")
            raw = work.tile([P, 512], F32, name="raw", tag="eg", bufs=3, align_bytes=64)
            nc.scalar.copy(
                out=raw[:].rearrange("b (i q) -> b i q", i=IR), in_=banks[(c, 0, rh)][:].rearrange("b (q i) -> b i q", i=IR)
            )
            nc.gpsimd.tensor_tensor(
                out=osb[c][:].rearrange("b (r q) -> b r q", q=128)[:, rh * IR : (rh + 1) * IR, 0:64],
                in0=raw[:].rearrange("b (i q) -> b i q", i=IR),
                in1=bias_c[c].rearrange("b (r q) -> b r q", q=128)[:, rh * IR : (rh + 1) * IR, 0:64],
                op=ALU.add,
            )

        def store_rows(c, r0, r1):
            dst = out.rearrange("b (rh c i) q -> c b rh (i q)", c=NCHUNK, i=IR)[c]
            if r1 - r0 == RC:
                nc.sync.dma_start(out=dst, in_=osb[c][:].rearrange("b (rh x) -> b rh x", rh=NRH))
            else:
                rh = r0 // IR
                nc.sync.dma_start(
                    out=dst[:, rh, (r0 - rh * IR) * 128 : (r1 - rh * IR) * 128], in_=osb[c][:, r0 * 128 : r1 * 128]
                )

        hg = {}

        def late_row(c):
            add_bias(c, 1)
            store_rows(c, 0, RC)

        load_bytes("E0")
        load_bytes("E1")
        load_bytes("L0")
        widen("E0")
        permute_bias()
        load_bytes("E2")
        early_interleave(0, 0)
        early_interleave(0, 1)
        widen("E1")
        load_bytes("L1")
        load_windows(0, (0,))
        widen("L0")
        early_quantize(0, 0)
        load_bytes("E3")
        load_windows(0, (1, 2))
        early_quantize(0, 1)
        early_interleave(1, 0)
        early_interleave(1, 1)
        widen("E2")
        load_bytes("L2")
        load_x(1, (0, 1))
        load_windows(0, (3,))
        early_quantize(1, 0)
        widen("L1")
        load_bytes("L3")
        load_windows(0, (4, 5, 6, 7))
        early_quantize(1, 1)
        early_interleave(2, 0)
        early_interleave(2, 1)
        widen("E3")
        load_bias(0)
        load_bias(1)
        early_quantize(2, 0)
        gather(1, 0)
        gather(1, 1)
        widen("L2")
        load_bias(2)
        early_quantize(2, 1)
        early_interleave(3, 0)
        widen("L3")
        hg[1] = turn(hw[1])
        hg[0] = turn(hw[0])
        load_bias(3)
        quantize_h(1, hg[1])
        quantize_h(0, hg[0])
        early_quantize(3, 0)
        late_tile(0)
        late_copy("scalar", 0, 0, 128)
        late_tile(1)
        late_copy("scalar", 1, 0, 96)
        late_copy("vector", 1, 96, 128)
        multiply(0, 0)
        add_bias(0, 0)
        multiply(1, 0)
        quantize(0)
        multiply(0, 1)
        add_bias(1, 0)
        late_row(0)
        late_tile(2)
        late_copy("gpsimd", 2, 80, 128)
        late_copy("scalar", 2, 0, 80)
        early_interleave(3, 1)
        multiply(2, 0)
        quantize(1)
        multiply(1, 1)
        add_bias(2, 0)
        late_row(1)
        late_tile(3)
        late_copy("gpsimd", 3, 80, 128)
        late_copy("scalar", 3, 0, 80)
        multiply(3, 0)
        quantize(2)
        multiply(2, 1)
        add_bias(3, 0)
        late_row(2)
        late_tile(4)
        late_copy("gpsimd", 4, 80, 128)
        late_copy("scalar", 4, 0, 80)
        early_quantize(3, 1)
        multiply(4, 0)
        quantize(3)
        multiply(3, 1)
        add_bias(4, 0)
        late_row(3)
        late_tile(5)
        late_copy("gpsimd", 5, 80, 128)
        late_copy("scalar", 5, 0, 80)
        multiply(5, 0)
        quantize(4)
        multiply(4, 1)
        add_bias(5, 0)
        late_row(4)
        late_tile(6)
        late_copy("gpsimd", 6, 80, 128)
        late_copy("scalar", 6, 0, 80)
        multiply(6, 0)
        multiply(7, 0)
        quantize(5)
        multiply(5, 1)
        add_bias(6, 0)
        late_row(5)
        late_tile(7)
        late_copy("gpsimd", 7, 80, 128)
        late_copy("scalar", 7, 0, 80)
        quantize(6)
        multiply(6, 1)
        quantize(7)
        multiply(7, 1)
        add_bank_side(7, 1)
        late_row(6)
        add_bank(7, 0, 0, 0, 16)
        add_bank(7, 1, 0, 0, 16)
        add_bank(7, 1, 1, 0, 8)
        store_rows(7, 0, 8)
        add_bank(7, 1, 1, 8, 16)
        store_rows(7, 8, 16)
